import numpy as np
import ml_dtypes


def mxq(x, axis, fmt="e4m3"):
    dtype, down = {"e4m3": (ml_dtypes.float8_e4m3fn, 7), "e5m2": (ml_dtypes.float8_e5m2, 14)}[fmt]
    v = np.moveaxis(np.asarray(x, np.float32).astype(ml_dtypes.bfloat16).astype(np.float64), axis, -1)
    blocks = v.reshape(v.shape[:-1] + (-1, 32))
    amax = np.abs(blocks).max(-1, keepdims=True)
    byte = np.maximum(np.where(amax > 0, np.frexp(amax)[1] - 1 + 127, 0) - down, 1)
    scale = np.exp2(byte - 127.0)
    codes = (blocks / scale).astype(np.float32).astype(dtype).astype(np.float64)
    return np.moveaxis((codes * scale).reshape(v.shape), -1, axis)


WIDE = False


def mx_kscale(k):
    if not WIDE:
        return np.ones(k)
    levels = np.array([10, -10, 5, -5, 0])
    if k % 512:
        return np.exp2(np.random.permutation(np.resize(levels, k // 32))).repeat(32)
    a = np.empty((k // 512, 16))
    for p in range(k // 512):
        a[p, :8] = np.random.permutation(np.resize(levels, 8))
        for g in range(8):
            far = levels[np.abs(levels - a[p, g]) >= 10]
            a[p, g + 8] = far[np.random.randint(len(far))]
    return np.exp2(a.ravel()).repeat(32)


BF16 = ml_dtypes.bfloat16


def bf(x):
    return np.asarray(x, np.float32).astype(BF16)


def f64(x):
    return np.asarray(x).astype(np.float64)


B, T, D, H, KH, F = 2, 128, 1024, 8, 2, 4096
EPS = 1e-5


def layer_norm(v, g, b):
    m = v.mean(-1, keepdims=True)
    var = ((v - m) ** 2).mean(-1, keepdims=True)
    return (v - m) / np.sqrt(var + EPS) * g + b


def draw0():
    s, t = mx_kscale(D), mx_kscale(D)
    return {
        "h_attn": bf(np.random.standard_normal((B, T, D)) * 0.4 * s),
        "x": bf(np.random.standard_normal((B, T, D))),
        "Wo": bf(np.random.standard_normal((D, D)) * 2.0 / np.sqrt(D) / s[:, None]),
        "bo": bf(np.random.standard_normal(D) * 0.2),
        "ln2_g": bf(1.5 + 0.3 * np.random.standard_normal(D)),
        "ln2_b": bf(0.3 + 0.3 * np.random.standard_normal(D)),
        "fln_g": bf((1.0 + 0.1 * np.random.standard_normal(D)) * t),
        "fln_b": bf(0.2 * np.random.standard_normal(D) * t),
        "W1": bf(np.random.standard_normal((D, F)) / np.sqrt(D) / t[:, None]),
        "b1": bf(np.random.standard_normal(F) * 0.3),
        "W2": bf(np.random.standard_normal((D, F)) / np.sqrt(D) / t[:, None]),
        "b2": bf(np.random.standard_normal(F) * 0.3),
    }


def core(h_attn, x, Wo, bo, ln2_g, ln2_b, fln_g, fln_b, W1, b1, W2, b2):
    y = f64(x) + ((mxq(f64(h_attn), 2, "e4m3") @ mxq(f64(Wo), 0, "e4m3")) + f64(bo))
    r = layer_norm(y, f64(ln2_g), f64(ln2_b))
    h2q = mxq(layer_norm(r, f64(fln_g), f64(fln_b)), 2, "e4m3")
    g_pre = (h2q @ mxq(f64(W1), 0, "e4m3")) + f64(b1)
    hidden = (h2q @ mxq(f64(W2), 0, "e4m3")) + f64(b2)
    return r, g_pre, hidden


def e4m3fn_bytes(y):
    return np.clip(np.asarray(y, np.float64), -448.0, 448.0).astype(np.float32).astype(ml_dtypes.float8_e4m3fn).view(np.uint8)


def e4m3fn_values(b):
    return np.asarray(b, np.uint8).view(ml_dtypes.float8_e4m3fn).astype(np.float64)


def setup_inputs():
    d = draw0()
    x0 = np.asarray(d['W2']).astype(np.float64)
    s = (np.max(np.abs(x0), axis=(1,), keepdims=True) / 448.0).astype(np.float32)
    out = {}
    for k, v in d.items():
        if k == 'W2':
            out['W2_bytes'] = e4m3fn_bytes(x0 / s.astype(np.float64))
            out['W2_scale'] = s
        else:
            out[k] = v
    return out


def reference(h_attn, x, Wo, bo, ln2_g, ln2_b, fln_g, fln_b, W1, b1, W2_bytes, W2_scale, b2):
    return core(h_attn, x, Wo, bo, ln2_g, ln2_b, fln_g, fln_b, W1, b1, e4m3fn_values(W2_bytes) * W2_scale.astype(np.float64), b2)

@@ -1,0 +1,281 @@
+from contextlib import ExitStack
+
+import concourse.mybir as mybir
+from concourse.masks import make_identity
+
+F32 = mybir.dt.float32
+BF16 = mybir.dt.bfloat16
+U32 = mybir.dt.uint32
+U8 = mybir.dt.uint8
+FP8 = mybir.dt.float8_e4m3fn
+FP8X4 = mybir.dt.float8_e4m3fn_x4
+ACT = mybir.ActivationFunctionType
+ALU = mybir.AluOpType
+
+P = 128
+PACK = 4
+D = 1024
+F = 4096
+TOK = 256
+G = 2
+CW = 512
+LW = 1024
+EPS = 1e-5
+
+FLOPS = 2 * TOK * D * (D + 2 * F)
+
+
+def tile_transformerblock_pa_kernel(
+    tc, h_attn, x, Wo, bo, ln2_g, ln2_b, fln_g, fln_b, W1, b1, W2_bytes, W2_scale, b2, out_0, out_1, out_2
+):
+    nc = tc.nc
+    with ExitStack() as ctx:
+        const = ctx.enter_context(tc.tile_pool(name="const", bufs=1))
+        work = ctx.enter_context(tc.tile_pool(name="work", bufs=2))
+        raws = ctx.enter_context(tc.tile_pool(name="raws", bufs=4))
+        byts = ctx.enter_context(tc.tile_pool(name="byts", bufs=4))
+        wides = ctx.enter_context(tc.tile_pool(name="wides", bufs=3))
+        ils = ctx.enter_context(tc.tile_pool(name="ils", bufs=3))
+        cods = ctx.enter_context(tc.tile_pool(name="cods", bufs=6))
+        ps_mm = ctx.enter_context(tc.psum_pool(name="ps_mm", bufs=4))
+        ps_tr = ctx.enter_context(tc.psum_pool(name="ps_tr", bufs=2))
+        ps_il = ctx.enter_context(tc.psum_pool(name="ps_il", bufs=2))
+
+        with tc.tile_pool(name="early", bufs=1) as early, tc.tile_pool(name="norm", bufs=2) as norm:
+            scale_t = const.tile([P, G, PACK], F32)
+            nc.scalar.dma_start(out=scale_t[:], in_=W2_scale.rearrange("(g p t) o -> p g (t o)", p=P, t=PACK))
+            fg_b = const.tile([P, G, PACK], BF16)
+            nc.scalar.dma_start(out=fg_b[:], in_=fln_g.rearrange("(g p t) -> p g t", p=P, t=PACK))
+            fb_b = const.tile([P, G, PACK], BF16)
+            nc.scalar.dma_start(out=fb_b[:], in_=fln_b.rearrange("(g p t) -> p g t", p=P, t=PACK))
+
+            w1_view = W1.rearrange("(g p t) n -> g p t n", p=P, t=PACK)
+            w2_view = W2_bytes.rearrange("(g p t) n -> g p t n", p=P, t=PACK)
+            wo_view = Wo.rearrange("(g p t) n -> g p t n", p=P, t=PACK)
+
+            w2_bytes = {}
+            w1_raw = {}
+
+            def load_w2(g, j):
+                t = byts.tile([P, PACK, LW], U8, name="w2b", align_bytes=64)
+                nc.sync.dma_start(out=t[:], in_=w2_view[g][:, :, j * LW : (j + 1) * LW])
+                w2_bytes[g, j] = t
+
+            def load_w1(g, j):
+                t = raws.tile([P, PACK, LW], BF16, name="raw", align_bytes=64)
+                nc.sync.dma_start(out=t[:], in_=w1_view[g][:, :, j * LW : (j + 1) * LW])
+                w1_raw[g, j] = t
+
+            h_sb = early.tile([P, 2, D], BF16)
+            nc.sync.dma_start(out=h_sb[:], in_=h_attn.rearrange("b t d -> t b d"))
+            wo_raw = []
+            for g in range(G):
+                wo_t = raws.tile([P, PACK, LW], BF16, name="raw", align_bytes=64)
+                nc.sync.dma_start(out=wo_t[:], in_=wo_view[g])
+                wo_raw.append(wo_t)
+                if g == 0:
+                    load_w2(0, 0)
+            x_sb = early.tile([P, 2, D], BF16)
+            nc.sync.dma_start(out=x_sb[:], in_=x.rearrange("b t d -> t b d"))
+            bo_sb = early.tile([P, D], BF16)
+            nc.sync.dma_start(out=bo_sb[:], in_=bo.partition_broadcast(P))
+            g2_sb = early.tile([P, D], BF16)
+            nc.sync.dma_start(out=g2_sb[:], in_=ln2_g.partition_broadcast(P))
+            b2_sb = early.tile([P, D], BF16)
+            nc.sync.dma_start(out=b2_sb[:], in_=ln2_b.partition_broadcast(P))
+            load_w2(1, 0)
+            load_w1(0, 0)
+            load_w1(1, 0)
+            bias = const.tile([P, 2, F], BF16)
+            nc.sync.dma_start(out=bias[:, 0, :], in_=b1.partition_broadcast(P))
+            nc.sync.dma_start(out=bias[:, 1, :], in_=b2.partition_broadcast(P))
+
+            ident = const.tile([P, P], F32)
+            make_identity(nc, ident[:])
+            ident_b = const.tile([P, P], BF16)
+            nc.vector.tensor_copy(out=ident_b[:], in_=ident[:])
+            fg = const.tile([P, G, PACK], F32)
+            nc.gpsimd.tensor_copy(out=fg[:], in_=fg_b[:])
+            fb = const.tile([P, G, PACK], F32)
+            nc.gpsimd.tensor_copy(out=fb[:], in_=fb_b[:])
+
+            def interleave(engine, dst, src):
+                o = dst.rearrange("p (c i t) -> p c t i", i=4, t=PACK)
+                i = src.rearrange("p t (c i) -> p c t i", i=4)
+                if engine == "V":
+                    nc.vector.tensor_copy(out=o, in_=i)
+                else:
+                    nc.scalar.copy(out=o, in_=i)
+
+            def interleave_pe(dst, src):
+                w = src.shape[2]
+                for q in range(w // 256):
+                    bank = ps_il.tile([P, 1024], BF16, name="bank")
+                    for s in range(2):
+                        cols = slice(q * 256 + s * 128, q * 256 + (s + 1) * 128)
+                        nc.tensor.matmul(
+                            bank[:, s * 512 : (s + 1) * 512],
+                            lhsT=ident_b[:],
+                            rhs=src[:, :, cols].rearrange("p t w -> p w t"),
+                            start=True,
+                            stop=True,
+                        )
+                    nc.scalar.copy(out=dst[:, q * 1024 : (q + 1) * 1024], in_=bank[:])
+
+            def quantize(codes, scales, src):
+                nc.vector.quantize_mx(out=codes.bitcast(FP8X4), scales=scales, in_=src)
+
+            def mx(acc, lc, ls, rc, rs, g):
+                nc.tensor.matmul_mx(
+                    out=acc,
+                    lhsT=lc.bitcast(FP8X4),
+                    lhsT_scale=ls,
+                    rhs=rc.bitcast(FP8X4),
+                    rhs_scale=rs,
+                    start=(g == 0),
+                    stop=(g == G - 1),
+                )
+
+            hq = early.tile([P, G, TOK], U32, align_bytes=64)
+            hs = early.tile([P, G, TOK], U8, align_bytes=64)
+            for g in range(G):
+                xt = ps_tr.tile([P, 2, TOK], F32, name="tr")
+                for m in range(2):
+                    words = h_sb[:, m, :].bitcast(F32)
+                    for u in range(2):
+                        nc.tensor.transpose(
+                            xt[:, u, m * P : (m + 1) * P], words[:, 256 * g + u : 256 * (g + 1) : 2], ident[:]
+                        )
+                hg = norm.tile([P, TOK * PACK], BF16, name="hg", align_bytes=64)
+                nc.vector.tensor_copy(
+                    out=hg[:].bitcast(F32).rearrange("p (r u) -> p r u", u=2), in_=xt[:].rearrange("p u r -> p r u")
+                )
+                quantize(hq[:, g, :], hs[:, g, :], hg[:])
+
+            xb = early.tile([P, 2, D], F32)
+            for m in range(2):
+                nc.vector.tensor_tensor(out=xb[:, m, :], in0=x_sb[:, m, :], in1=bo_sb[:], op=ALU.add)
+
+            woq = early.tile([P, G, D], U32, align_bytes=64)
+            wos = early.tile([P, G, D], U8, align_bytes=64)
+            for g in range(G):
+                for c in range(2):
+                    il = norm.tile([P, CW * PACK], BF16, name="ilo", align_bytes=64)
+                    cols = slice(c * CW, (c + 1) * CW)
+                    interleave("VS"[c], il[:], wo_raw[g][:, :, cols])
+                    quantize(woq[:, g, cols], wos[:, g, cols], il[:])
+
+            def rstd(mv, name):
+                ve = work.tile([P, 1], F32, name="ve" + name)
+                nc.vector.tensor_scalar(out=ve[:], in0=mv[:, 1:2], scalar1=EPS, scalar2=None, op0=ALU.add)
+                rs = work.tile([P, 1], F32, name="rs" + name)
+                nc.scalar.activation(out=rs[:], in_=ve[:], func=ACT.Abs_reciprocal_sqrt)
+                return rs
+
+            def stats(src, name):
+                st = work.tile([P, 2, 6], F32, name="st" + name)
+                for n in range(2):
+                    nc.vector.bn_stats(out=st[:, n, :], in_=src[:, n * 512 : (n + 1) * 512])
+                mv = work.tile([P, 2], F32, name="mv" + name)
+                nc.vector.bn_aggr(out=mv[:], in_=st[:].rearrange("p n s -> p (n s)"))
+                return mv
+
+            zs = []
+            for m in range(2):
+                y = xb[:, m, :]
+                for n in range(2):
+                    acc = ps_mm.tile([P, 512], F32, name="acc")
+                    cols = slice(n * 512, (n + 1) * 512)
+                    for g in range(G):
+                        mx(acc[:], hq[:, g, m * P : (m + 1) * P], hs[:, g, m * P : (m + 1) * P], woq[:, g, cols], wos[:, g, cols], g)
+                    nc.vector.tensor_tensor(out=y[:, cols], in0=acc[:], in1=xb[:, m, cols], op=ALU.add)
+                mv = stats(y, "a")
+                rs = rstd(mv, "a")
+                r = norm.tile([P, D], F32, name="r")
+                nc.vector.scalar_tensor_tensor(out=y, in0=y, scalar=mv[:, 0:1], in1=g2_sb[:], op0=ALU.subtract, op1=ALU.mult)
+                nc.vector.scalar_tensor_tensor(out=r[:], in0=y, scalar=rs[:], in1=b2_sb[:], op0=ALU.mult, op1=ALU.add)
+                nc.sync.dma_start(out=out_0[m], in_=r[:])
+                mv2 = stats(r, "b")
+                rs2 = rstd(mv2, "b")
+                nb = work.tile([P, 1], F32, name="nb")
+                nc.vector.scalar_tensor_tensor(
+                    out=nb[:], in0=mv2[:, 0:1], scalar=-1.0, in1=rs2[:], op0=ALU.mult, op1=ALU.mult
+                )
+                z = norm.tile([P, G, PACK, P], F32, name="z")
+                nc.scalar.activation(
+                    out=z[:],
+                    in_=r[:].rearrange("p (g q t) -> p g t q", g=G, t=PACK),
+                    func=ACT.Identity,
+                    scale=rs2[:],
+                    bias=nb[:],
+                )
+                zs.append(z)
+
+            h2q = const.tile([P, G, TOK], U32, align_bytes=64)
+            h2s = const.tile([P, G, TOK], U8, align_bytes=64)
+            for g in range(G):
+                hT = work.tile([P, PACK, TOK], BF16, name="hT", align_bytes=64)
+                for tp in range(2):
+                    zt = ps_tr.tile([P, 2, TOK], F32, name="tr")
+                    for m in range(2):
+                        for u in range(2):
+                            nc.tensor.transpose(zt[:, u, m * P : (m + 1) * P], zs[m][:, g, tp * 2 + u, :], ident[:])
+                    for u in range(2):
+                        t = tp * 2 + u
+                        nc.scalar.activation(
+                            out=hT[:, t, :],
+                            in_=zt[:, u, :],
+                            func=ACT.Identity,
+                            scale=fg[:, g, t : t + 1],
+                            bias=fb[:, g, t : t + 1],
+                        )
+                hi = work.tile([P, TOK * PACK], BF16, name="hi", align_bytes=64)
+                interleave("V", hi[:], hT[:])
+                quantize(h2q[:, g, :], h2s[:, g, :], hi[:])
+
+        outs = ctx.enter_context(tc.tile_pool(name="outs", bufs=8))
+
+        out_dram = (out_1, out_2)
+        for j in range(F // LW):
+            if j > 0:
+                for g in range(G):
+                    load_w2(g, j)
+                for g in range(G):
+                    load_w1(g, j)
+            for cc in range(LW // CW):
+                c = j * (LW // CW) + cc
+                lcols = slice(cc * CW, (cc + 1) * CW)
+                for w in (1, 0):
+                    q = cods.tile([P, G, CW], U32, name="q%d" % w, align_bytes=64)
+                    s = cods.tile([P, G, CW], U8, name="s%d" % w, align_bytes=64)
+                    pair = ils.tile([P, G, CW * PACK], BF16, name="il", align_bytes=64)
+                    for g in range(G):
+                        il = pair[:, g, :]
+                        if w == 1:
+                            wide = wides.tile([P, PACK, CW], BF16, name="wide", align_bytes=64)
+                            for t in range(PACK):
+                                nc.scalar.activation(
+                                    out=wide[:, t, :],
+                                    in_=w2_bytes[g, j][:, t, lcols].bitcast(FP8),
+                                    func=ACT.Copy,
+                                    scale=scale_t[:, g, t : t + 1],
+                                )
+                            interleave("V", il, wide[:])
+                        elif g == 0 or c == 7:
+                            interleave("S", il, w1_raw[g, j][:, :, lcols])
+                        else:
+                            interleave_pe(il, w1_raw[g, j][:, :, lcols])
+                    quantize(
+                        q[:].rearrange("p g c -> p (g c)"),
+                        s[:].rearrange("p g c -> p (g c)"),
+                        pair[:].rearrange("p g c -> p (g c)"),
+                    )
+                    for m in range(2):
+                        acc = ps_mm.tile([P, 512], F32, name="acc")
+                        for g in range(G):
+                            mx(acc[:], h2q[:, g, m * P : (m + 1) * P], h2s[:, g, m * P : (m + 1) * P], q[:, g, :], s[:, g, :], g)
+                        ot = outs.tile([P, CW], F32, name="ot")
+                        nc.vector.tensor_tensor(
+                            out=ot[:], in0=acc[:], in1=bias[:, w, c * CW : (c + 1) * CW], op=ALU.add
+                        )
+                        nc.sync.dma_start(out=out_dram[w][m][:, c * CW : (c + 1) * CW], in_=ot[:])

@@ -19,10 +19,21 @@ F = 4096
 TOK = 256
 G = 2
 CW = 512
+NC_ = F // CW
+EARLY_C = 3
 LW = 1024
 EPS = 1e-5
 
 FLOPS = 2 * TOK * D * (D + 2 * F)
+
+AHEAD = 12
+N_A = 8
+N_B = 8
+V_A = 0
+V_B = 1
+V_C = 2
+W1_PE = 11
+W1_S = 13
 
 
 def tile_transformerblock_pa_kernel(
@@ -34,16 +45,23 @@ def tile_transformerblock_pa_kernel(
         work = ctx.enter_context(tc.tile_pool(name="work", bufs=2))
         raws = ctx.enter_context(tc.tile_pool(name="raws", bufs=4))
         byts = ctx.enter_context(tc.tile_pool(name="byts", bufs=4))
-        wides = ctx.enter_context(tc.tile_pool(name="wides", bufs=3))
-        ils = ctx.enter_context(tc.tile_pool(name="ils", bufs=3))
-        cods = ctx.enter_context(tc.tile_pool(name="cods", bufs=6))
+        wides = ctx.enter_context(tc.tile_pool(name="wides", bufs=4))
+        ils = ctx.enter_context(tc.tile_pool(name="ils", bufs=2))
+        cods = ctx.enter_context(tc.tile_pool(name="cods", bufs=EARLY_C))
         ps_mm = ctx.enter_context(tc.psum_pool(name="ps_mm", bufs=4))
         ps_tr = ctx.enter_context(tc.psum_pool(name="ps_tr", bufs=2))
         ps_il = ctx.enter_context(tc.psum_pool(name="ps_il", bufs=2))
+        ctx.enter_context(tc.manual_schedule())
 
-        with tc.tile_pool(name="early", bufs=1) as early, tc.tile_pool(name="norm", bufs=2) as norm:
+        with tc.tile_pool(name="early", bufs=1) as early:
+            vec = const.tile([P, 512], BF16)
+            nc.vector.memset(vec[:], 0.0)
+            ident = const.tile([P, P], F32)
+            make_identity(nc, ident[:])
             scale_t = const.tile([P, G, PACK], F32)
             nc.scalar.dma_start(out=scale_t[:], in_=W2_scale.rearrange("(g p t) o -> p g (t o)", p=P, t=PACK))
+            for i, v in enumerate((bo, ln2_g, ln2_b)):
+                nc.scalar.dma_start(out=vec[2 * i : 2 * i + 2, :], in_=v.rearrange("(r c) -> r c", c=512))
             fg_b = const.tile([P, G, PACK], BF16)
             nc.scalar.dma_start(out=fg_b[:], in_=fln_g.rearrange("(g p t) -> p g t", p=P, t=PACK))
             fb_b = const.tile([P, G, PACK], BF16)
@@ -52,7 +70,6 @@ def tile_transformerblock_pa_kernel(
             w1_view = W1.rearrange("(g p t) n -> g p t n", p=P, t=PACK)
             w2_view = W2_bytes.rearrange("(g p t) n -> g p t n", p=P, t=PACK)
             wo_view = Wo.rearrange("(g p t) n -> g p t n", p=P, t=PACK)
-
             w2_bytes = {}
             w1_raw = {}
 
@@ -68,30 +85,31 @@ def tile_transformerblock_pa_kernel(
 
             h_sb = early.tile([P, 2, D], BF16)
             nc.sync.dma_start(out=h_sb[:], in_=h_attn.rearrange("b t d -> t b d"))
-            wo_raw = []
-            for g in range(G):
-                wo_t = raws.tile([P, PACK, LW], BF16, name="raw", align_bytes=64)
-                nc.sync.dma_start(out=wo_t[:], in_=wo_view[g])
-                wo_raw.append(wo_t)
-                if g == 0:
-                    load_w2(0, 0)
+            wo_raw = {}
+
+            def load_wo(g, c):
+                t = early.tile([P, PACK, CW], BF16, name="wo%d%d" % (g, c), align_bytes=64)
+                nc.sync.dma_start(out=t[:], in_=wo_view[g][:, :, c * CW : (c + 1) * CW])
+                wo_raw[g, c] = t
+
+            load_wo(0, 0)
+            load_w2(0, 0)
+            load_wo(1, 0)
+            load_wo(0, 1)
+            load_wo(1, 1)
             x_sb = early.tile([P, 2, D], BF16)
             nc.sync.dma_start(out=x_sb[:], in_=x.rearrange("b t d -> t b d"))
-            bo_sb = early.tile([P, D], BF16)
-            nc.sync.dma_start(out=bo_sb[:], in_=bo.partition_broadcast(P))
-            g2_sb = early.tile([P, D], BF16)
-            nc.sync.dma_start(out=g2_sb[:], in_=ln2_g.partition_broadcast(P))
-            b2_sb = early.tile([P, D], BF16)
-            nc.sync.dma_start(out=b2_sb[:], in_=ln2_b.partition_broadcast(P))
             load_w2(1, 0)
             load_w1(0, 0)
             load_w1(1, 0)
+            load_w2(0, 1)
+            load_w2(1, 1)
             bias = const.tile([P, 2, F], BF16)
             nc.sync.dma_start(out=bias[:, 0, :], in_=b1.partition_broadcast(P))
             nc.sync.dma_start(out=bias[:, 1, :], in_=b2.partition_broadcast(P))
+            load_w1(0, 1)
+            load_w1(1, 1)
 
-            ident = const.tile([P, P], F32)
-            make_identity(nc, ident[:])
             ident_b = const.tile([P, P], BF16)
             nc.vector.tensor_copy(out=ident_b[:], in_=ident[:])
             fg = const.tile([P, G, PACK], F32)
@@ -107,37 +125,109 @@ def tile_transformerblock_pa_kernel(
                 else:
                     nc.scalar.copy(out=o, in_=i)
 
-            def interleave_pe(dst, src):
-                w = src.shape[2]
-                for q in range(w // 256):
-                    bank = ps_il.tile([P, 1024], BF16, name="bank")
-                    for s in range(2):
-                        cols = slice(q * 256 + s * 128, q * 256 + (s + 1) * 128)
-                        nc.tensor.matmul(
-                            bank[:, s * 512 : (s + 1) * 512],
-                            lhsT=ident_b[:],
-                            rhs=src[:, :, cols].rearrange("p t w -> p w t"),
-                            start=True,
-                            stop=True,
-                        )
-                    nc.scalar.copy(out=dst[:, q * 1024 : (q + 1) * 1024], in_=bank[:])
-
             def quantize(codes, scales, src):
                 nc.vector.quantize_mx(out=codes.bitcast(FP8X4), scales=scales, in_=src)
 
             def mx(acc, lc, ls, rc, rs, g):
                 nc.tensor.matmul_mx(
-                    out=acc,
-                    lhsT=lc.bitcast(FP8X4),
-                    lhsT_scale=ls,
-                    rhs=rc.bitcast(FP8X4),
-                    rhs_scale=rs,
-                    start=(g == 0),
-                    stop=(g == G - 1),
+                    out=acc, lhsT=lc.bitcast(FP8X4), lhsT_scale=ls, rhs=rc.bitcast(FP8X4), rhs_scale=rs,
+                    start=(g == 0), stop=(g == G - 1),
                 )
+
+            q = {}
+            s = {}
+            pair = {}
+            wide = {}
+            s_steps = []
+            v_steps = []
+
+            def w_new(w, c):
+                pair[w, c] = ils.tile([P, G, CW * PACK], BF16, name="il%d" % w, align_bytes=64)
+
+            def do_widen(c, g, t):
+                if t == 0:
+                    wide[c, g] = wides.tile([P, PACK, CW], BF16, name="wide", align_bytes=64)
+                cols = slice((c % 2) * CW, (c % 2 + 1) * CW)
+                nc.scalar.activation(
+                    out=wide[c, g][:, t, :], in_=w2_bytes[g, c // 2][:, t, cols].bitcast(FP8), func=ACT.Copy,
+                    scale=scale_t[:, g, t : t + 1],
+                )
+
+            def do_il1(c, g, half):
+                if g == 0 and half == 0:
+                    w_new(0, c)
+                base = (c % 2) * CW + half * 256
+                dst = pair[0, c][:, g, half * 1024 : (half + 1) * 1024]
+                src = w1_raw[g, c // 2][:, :, base : base + 256]
+                n = 2 * c + half
+                if g == 1 and n < W1_PE:
+                    bank = ps_il.tile([P, 1024], BF16, name="bank")
+                    for k in range(2):
+                        nc.tensor.matmul(
+                            bank[:, k * 512 : (k + 1) * 512], lhsT=ident_b[:],
+                            rhs=src[:, :, k * 128 : (k + 1) * 128].rearrange("p t w -> p w t"), start=True, stop=True,
+                        )
+                    nc.scalar.copy(out=dst, in_=bank[:])
+                else:
+                    interleave("V" if g == 1 and n >= W1_S else "S", dst, src)
+
+            def load_pair(c, load):
+                for g in range(G):
+                    load(g, c // 2 + 2)
+
+            def do_il2(c, g):
+                if g == 0:
+                    w_new(1, c)
+                interleave("V", pair[1, c][:, g, :], wide[c, g][:])
+
+            def do_q(w, c):
+                pool = cods if c < EARLY_C else late
+                q[w, c] = pool.tile([P, G, CW], U32, name="q%d" % w, align_bytes=64)
+                s[w, c] = pool.tile([P, G, CW], U8, name="s%d" % w, align_bytes=64)
+                quantize(
+                    q[w, c][:].rearrange("p g c -> p (g c)"), s[w, c][:].rearrange("p g c -> p (g c)"),
+                    pair[w, c][:].rearrange("p g c -> p (g c)"),
+                )
+
+            for c in range(NC_):
+                for g in range(G):
+                    for t in range(PACK):
+                        s_steps.append((do_widen, c, g, t))
+                    v_steps.append((len(s_steps), do_il2, c, g))
+                if c % 2 == 1 and c // 2 + 2 < F // LW:
+                    s_steps.append((load_pair, c, load_w2))
+                v_steps.append((len(s_steps), do_q, 1, c))
+                for g in range(G):
+                    for half in range(2):
+                        if g == 0 or 2 * c + half < W1_S:
+                            s_steps.append((do_il1, c, g, half))
+                for half in range(2):
+                    if 2 * c + half >= W1_S:
+                        v_steps.append((len(s_steps), do_il1, c, 1, half))
+                if c % 2 == 1 and c // 2 + 2 < F // LW:
+                    s_steps.append((load_pair, c, load_w1))
+                v_steps.append((len(s_steps), do_q, 0, c))
+
+            done = {"s": 0, "v": 0}
+
+            def advance_s(n):
+                for k in range(n):
+                    if done["s"] < len(s_steps):
+                        step = s_steps[done["s"]]
+                        done["s"] += 1
+                        step[0](*step[1:])
+
+            def advance_v(n, ahead=0):
+                for k in range(n):
+                    if done["v"] < len(v_steps):
+                        step = v_steps[done["v"]]
+                        done["v"] += 1
+                        advance_s(step[0] + ahead - done["s"])
+                        step[1](*step[2:])
 
             hq = early.tile([P, G, TOK], U32, align_bytes=64)
             hs = early.tile([P, G, TOK], U8, align_bytes=64)
+            hgs = []
             for g in range(G):
                 xt = ps_tr.tile([P, 2, TOK], F32, name="tr")
                 for m in range(2):
@@ -146,41 +236,60 @@ def tile_transformerblock_pa_kernel(
                         nc.tensor.transpose(
                             xt[:, u, m * P : (m + 1) * P], words[:, 256 * g + u : 256 * (g + 1) : 2], ident[:]
                         )
-                hg = norm.tile([P, TOK * PACK], BF16, name="hg", align_bytes=64)
+                hg = early.tile([P, TOK * PACK], BF16, name="hg%d" % g, align_bytes=64)
                 nc.vector.tensor_copy(
                     out=hg[:].bitcast(F32).rearrange("p (r u) -> p r u", u=2), in_=xt[:].rearrange("p u r -> p r u")
                 )
-                quantize(hq[:, g, :], hs[:, g, :], hg[:])
+                hgs.append(hg)
+            for g in range(G):
+                quantize(hq[:, g, :], hs[:, g, :], hgs[g][:])
 
-            xb = early.tile([P, 2, D], F32)
-            for m in range(2):
-                nc.vector.tensor_tensor(out=xb[:, m, :], in0=x_sb[:, m, :], in1=bo_sb[:], op=ALU.add)
+            rows = []
+            for i in range(3):
+                bank = ps_il.tile([P, 1024], BF16, name="bank")
+                for k in range(2):
+                    nc.tensor.matmul(
+                        bank[:, k * 512 : (k + 1) * 512],
+                        lhsT=ident_b[:, 2 * i + k : 2 * i + k + 1].to_broadcast([P, P]), rhs=vec[:], start=True, stop=True,
+                    )
+                row = early.tile([P, D], BF16, name="row%d" % i)
+                nc.scalar.copy(out=row[:], in_=bank[:])
+                rows.append(row)
+            bo_sb, g2_sb, b2_sb = rows
 
             woq = early.tile([P, G, D], U32, align_bytes=64)
             wos = early.tile([P, G, D], U8, align_bytes=64)
+            xb = early.tile([P, 2, D], F32)
+            wo_il = []
             for g in range(G):
-                for c in range(2):
-                    il = norm.tile([P, CW * PACK], BF16, name="ilo", align_bytes=64)
-                    cols = slice(c * CW, (c + 1) * CW)
-                    interleave("VS"[c], il[:], wo_raw[g][:, :, cols])
-                    quantize(woq[:, g, cols], wos[:, g, cols], il[:])
+                pair_o = ils.tile([P, G, CW * PACK], BF16, name="il%d" % g, align_bytes=64)
+                wo_il.append(pair_o)
+            interleave("V", wo_il[0][:, 0, :], wo_raw[0, 0][:])
+            advance_s(4)
+            interleave("V", wo_il[1][:, 0, :], wo_raw[1, 0][:])
+            interleave("V", wo_il[0][:, 1, :], wo_raw[0, 1][:])
+            interleave("S", wo_il[1][:, 1, :], wo_raw[1, 1][:])
+            for g in range(G):
+                nc.vector.tensor_tensor(out=xb[:, g, :], in0=x_sb[:, g, :], in1=bo_sb[:], op=ALU.add)
+                quantize(woq[:, g, :], wos[:, g, :], wo_il[g][:].rearrange("p g c -> p (g c)"))
 
-            def rstd(mv, name):
-                ve = work.tile([P, 1], F32, name="ve" + name)
-                nc.vector.tensor_scalar(out=ve[:], in0=mv[:, 1:2], scalar1=EPS, scalar2=None, op0=ALU.add)
-                rs = work.tile([P, 1], F32, name="rs" + name)
+            def sum_sq(src, m, nm, ss):
+                sq = early.tile([P, D], F32, name="sq")
+                nc.scalar.activation(
+                    out=sq[:], in_=src, func=ACT.Square, bias=nm[:, m : m + 1], accum_out=ss[:, m : m + 1]
+                )
+
+            def rstd(ss, name):
+                ve = early.tile([P, 2], F32, name="ve" + name)
+                nc.vector.tensor_scalar(out=ve[:], in0=ss[:], scalar1=1.0 / D, scalar2=EPS, op0=ALU.mult, op1=ALU.add)
+                rs = early.tile([P, 2], F32, name="rs" + name)
                 nc.scalar.activation(out=rs[:], in_=ve[:], func=ACT.Abs_reciprocal_sqrt)
                 return rs
 
-            def stats(src, name):
-                st = work.tile([P, 2, 6], F32, name="st" + name)
-                for n in range(2):
-                    nc.vector.bn_stats(out=st[:, n, :], in_=src[:, n * 512 : (n + 1) * 512])
-                mv = work.tile([P, 2], F32, name="mv" + name)
-                nc.vector.bn_aggr(out=mv[:], in_=st[:].rearrange("p n s -> p (n s)"))
-                return mv
-
-            zs = []
+            rr = []
+            sums = early.tile([P, 2, 2], F32)
+            nm1 = early.tile([P, 2], F32)
+            ss1 = early.tile([P, 2], F32)
             for m in range(2):
                 y = xb[:, m, :]
                 for n in range(2):
@@ -188,31 +297,56 @@ def tile_transformerblock_pa_kernel(
                     cols = slice(n * 512, (n + 1) * 512)
                     for g in range(G):
                         mx(acc[:], hq[:, g, m * P : (m + 1) * P], hs[:, g, m * P : (m + 1) * P], woq[:, g, cols], wos[:, g, cols], g)
-                    nc.vector.tensor_tensor(out=y[:, cols], in0=acc[:], in1=xb[:, m, cols], op=ALU.add)
-                mv = stats(y, "a")
-                rs = rstd(mv, "a")
-                r = norm.tile([P, D], F32, name="r")
-                nc.vector.scalar_tensor_tensor(out=y, in0=y, scalar=mv[:, 0:1], in1=g2_sb[:], op0=ALU.subtract, op1=ALU.mult)
-                nc.vector.scalar_tensor_tensor(out=r[:], in0=y, scalar=rs[:], in1=b2_sb[:], op0=ALU.mult, op1=ALU.add)
-                nc.sync.dma_start(out=out_0[m], in_=r[:])
-                mv2 = stats(r, "b")
-                rs2 = rstd(mv2, "b")
-                nb = work.tile([P, 1], F32, name="nb")
+                    nc.vector.scalar_tensor_tensor(
+                        out=y[:, cols], in0=acc[:], scalar=1.0, in1=xb[:, m, cols], op0=ALU.mult, op1=ALU.add,
+                        accum_out=sums[:, n, m : m + 1],
+                    )
+            half = early.tile([P, 2], F32)
+            nc.vector.tensor_tensor(out=half[:], in0=sums[:, 0, :], in1=sums[:, 1, :], op=ALU.add)
+            nc.vector.tensor_scalar(out=nm1[:], in0=half[:], scalar1=-1.0 / D, scalar2=None, op0=ALU.mult)
+            advance_s(N_A)
+            for m in range(2):
+                sum_sq(xb[:, m, :], m, nm1, ss1)
+            for m in range(2):
+                y = xb[:, m, :]
+                t = early.tile([P, D], F32, name="t%d" % m)
                 nc.vector.scalar_tensor_tensor(
-                    out=nb[:], in0=mv2[:, 0:1], scalar=-1.0, in1=rs2[:], op0=ALU.mult, op1=ALU.mult
+                    out=t[:], in0=y, scalar=nm1[:, m : m + 1], in1=g2_sb[:], op0=ALU.add, op1=ALU.mult
                 )
-                z = norm.tile([P, G, PACK, P], F32, name="z")
+                rr.append(t)
+            rs1 = rstd(ss1, "a")
+            sumr = early.tile([P, 2], F32)
+            nm2 = early.tile([P, 2], F32)
+            ss2 = early.tile([P, 2], F32)
+            advance_v(V_A)
+            for m in range(2):
+                r = rr[m][:]
+                nc.vector.scalar_tensor_tensor(
+                    out=r, in0=r, scalar=rs1[:, m : m + 1], in1=b2_sb[:], op0=ALU.mult, op1=ALU.add,
+                    accum_out=sumr[:, m : m + 1],
+                )
+                nc.sync.dma_start(out=out_0[m], in_=r)
+            nc.vector.tensor_scalar(out=nm2[:], in0=sumr[:], scalar1=-1.0 / D, scalar2=None, op0=ALU.mult)
+            advance_s(N_B)
+            for m in range(2):
+                sum_sq(rr[m][:], m, nm2, ss2)
+            advance_v(V_B)
+            rs2 = rstd(ss2, "b")
+            nb = early.tile([P, 2], F32)
+            nc.vector.tensor_tensor(out=nb[:], in0=nm2[:], in1=rs2[:], op=ALU.mult)
+            zs = []
+            for m in range(2):
+                z = xb[:, m, :].rearrange("p (g t q) -> p g t q", g=G, t=PACK)
                 nc.scalar.activation(
-                    out=z[:],
-                    in_=r[:].rearrange("p (g q t) -> p g t q", g=G, t=PACK),
-                    func=ACT.Identity,
-                    scale=rs2[:],
-                    bias=nb[:],
+                    out=z, in_=rr[m][:].rearrange("p (g q t) -> p g t q", g=G, t=PACK), func=ACT.Identity,
+                    scale=rs2[:, m : m + 1], bias=nb[:, m : m + 1],
                 )
                 zs.append(z)
+            advance_v(V_C)
 
             h2q = const.tile([P, G, TOK], U32, align_bytes=64)
             h2s = const.tile([P, G, TOK], U8, align_bytes=64)
+            his = []
             for g in range(G):
                 hT = work.tile([P, PACK, TOK], BF16, name="hT", align_bytes=64)
                 for tp in range(2):
@@ -223,59 +357,35 @@ def tile_transformerblock_pa_kernel(
                     for u in range(2):
                         t = tp * 2 + u
                         nc.scalar.activation(
-                            out=hT[:, t, :],
-                            in_=zt[:, u, :],
-                            func=ACT.Identity,
-                            scale=fg[:, g, t : t + 1],
-                            bias=fb[:, g, t : t + 1],
+                            out=hT[:, t, :], in_=zt[:, u, :], func=ACT.Identity, scale=fg[:, g, t : t + 1], bias=fb[:, g, t : t + 1],
                         )
+                advance_v(1)
                 hi = work.tile([P, TOK * PACK], BF16, name="hi", align_bytes=64)
                 interleave("V", hi[:], hT[:])
-                quantize(h2q[:, g, :], h2s[:, g, :], hi[:])
+                his.append(hi)
+            for g in range(G):
+                quantize(h2q[:, g, :], h2s[:, g, :], his[g][:])
 
         outs = ctx.enter_context(tc.tile_pool(name="outs", bufs=8))
-
+        late = ctx.enter_context(tc.tile_pool(name="late", bufs=4))
         out_dram = (out_1, out_2)
-        for j in range(F // LW):
-            if j > 0:
-                for g in range(G):
-                    load_w2(g, j)
-                for g in range(G):
-                    load_w1(g, j)
-            for cc in range(LW // CW):
-                c = j * (LW // CW) + cc
-                lcols = slice(cc * CW, (cc + 1) * CW)
-                for w in (1, 0):
-                    q = cods.tile([P, G, CW], U32, name="q%d" % w, align_bytes=64)
-                    s = cods.tile([P, G, CW], U8, name="s%d" % w, align_bytes=64)
-                    pair = ils.tile([P, G, CW * PACK], BF16, name="il", align_bytes=64)
-                    for g in range(G):
-                        il = pair[:, g, :]
-                        if w == 1:
-                            wide = wides.tile([P, PACK, CW], BF16, name="wide", align_bytes=64)
-                            for t in range(PACK):
-                                nc.scalar.activation(
-                                    out=wide[:, t, :],
-                                    in_=w2_bytes[g, j][:, t, lcols].bitcast(FP8),
-                                    func=ACT.Copy,
-                                    scale=scale_t[:, g, t : t + 1],
-                                )
-                            interleave("V", il, wide[:])
-                        elif g == 0 or c == 7:
-                            interleave("S", il, w1_raw[g, j][:, :, lcols])
-                        else:
-                            interleave_pe(il, w1_raw[g, j][:, :, lcols])
-                    quantize(
-                        q[:].rearrange("p g c -> p (g c)"),
-                        s[:].rearrange("p g c -> p (g c)"),
-                        pair[:].rearrange("p g c -> p (g c)"),
-                    )
-                    for m in range(2):
-                        acc = ps_mm.tile([P, 512], F32, name="acc")
-                        for g in range(G):
-                            mx(acc[:], h2q[:, g, m * P : (m + 1) * P], h2s[:, g, m * P : (m + 1) * P], q[:, g, :], s[:, g, :], g)
-                        ot = outs.tile([P, CW], F32, name="ot")
-                        nc.vector.tensor_tensor(
-                            out=ot[:], in0=acc[:], in1=bias[:, w, c * CW : (c + 1) * CW], op=ALU.add
-                        )
-                        nc.sync.dma_start(out=out_dram[w][m][:, c * CW : (c + 1) * CW], in_=ot[:])
+
+        def do_out(w, c, m):
+            acc = ps_mm.tile([P, 512], F32, name="acc")
+            for g in range(G):
+                mx(acc[:], h2q[:, g, m * P : (m + 1) * P], h2s[:, g, m * P : (m + 1) * P], q[w, c][:, g, :], s[w, c][:, g, :], g)
+            ot = outs.tile([P, CW], F32, name="ot")
+            nc.vector.tensor_tensor(out=ot[:], in0=acc[:], in1=bias[:, w, c * CW : (c + 1) * CW], op=ALU.add)
+            nc.sync.dma_start(out=out_dram[w][m][:, c * CW : (c + 1) * CW], in_=ot[:])
+
+        todo = [(do_out, w, c, m) for c in range(NC_) for w in (1, 0) for m in range(2)]
+        ready = []
+        while todo:
+            advance_v(1, AHEAD)
+            n = 0
+            more = done["v"] < len(v_steps)
+            while todo and n < (2 if more else 4) and (todo[0][1], todo[0][2]) in ready:
+                todo[0][0](*todo[0][1:])
+                todo.pop(0)
+                n += 1
+            ready = list(q)

@@ -27,13 +27,15 @@ EPS = 1e-5
 FLOPS = 2 * TOK * D * (D + 2 * F)
 
 AHEAD = 12
-N_A = 8
-N_B = 8
+N_BACK = 4
+N_0 = 4
+N_A = 14
+N_B = 3
 V_A = 0
-V_B = 1
+V_B = 2
 V_C = 2
-W1_PE = 11
-W1_S = 13
+W1_PE = 14
+W1_S = 15
 
 
 def tile_transformerblock_pa_kernel(
@@ -43,8 +45,8 @@ def tile_transformerblock_pa_kernel(
     with ExitStack() as ctx:
         const = ctx.enter_context(tc.tile_pool(name="const", bufs=1))
         work = ctx.enter_context(tc.tile_pool(name="work", bufs=2))
-        raws = ctx.enter_context(tc.tile_pool(name="raws", bufs=4))
-        byts = ctx.enter_context(tc.tile_pool(name="byts", bufs=4))
+        raws = ctx.enter_context(tc.tile_pool(name="raws", bufs=8))
+        byts = ctx.enter_context(tc.tile_pool(name="byts", bufs=6))
         wides = ctx.enter_context(tc.tile_pool(name="wides", bufs=4))
         ils = ctx.enter_context(tc.tile_pool(name="ils", bufs=2))
         cods = ctx.enter_context(tc.tile_pool(name="cods", bufs=EARLY_C))
@@ -54,14 +56,10 @@ def tile_transformerblock_pa_kernel(
         ctx.enter_context(tc.manual_schedule())
 
         with tc.tile_pool(name="early", bufs=1) as early:
-            vec = const.tile([P, 512], BF16)
-            nc.vector.memset(vec[:], 0.0)
             ident = const.tile([P, P], F32)
             make_identity(nc, ident[:])
             scale_t = const.tile([P, G, PACK], F32)
             nc.scalar.dma_start(out=scale_t[:], in_=W2_scale.rearrange("(g p t) o -> p g (t o)", p=P, t=PACK))
-            for i, v in enumerate((bo, ln2_g, ln2_b)):
-                nc.scalar.dma_start(out=vec[2 * i : 2 * i + 2, :], in_=v.rearrange("(r c) -> r c", c=512))
             fg_b = const.tile([P, G, PACK], BF16)
             nc.scalar.dma_start(out=fg_b[:], in_=fln_g.rearrange("(g p t) -> p g t", p=P, t=PACK))
             fb_b = const.tile([P, G, PACK], BF16)
@@ -73,16 +71,18 @@ def tile_transformerblock_pa_kernel(
             w2_bytes = {}
             w1_raw = {}
 
-            def load_w2(g, j):
-                t = byts.tile([P, PACK, LW], U8, name="w2b", align_bytes=64)
-                nc.sync.dma_start(out=t[:], in_=w2_view[g][:, :, j * LW : (j + 1) * LW])
-                w2_bytes[g, j] = t
+            def load_w2(g, c, n=2):
+                t = byts.tile([P, PACK, n * CW], U8, name="w2b", align_bytes=64)
+                nc.sync.dma_start(out=t[:], in_=w2_view[g][:, :, c * CW : (c + n) * CW])
+                for k in range(n):
+                    w2_bytes[g, c + k] = t[:, :, k * CW : (k + 1) * CW]
 
-            def load_w1(g, j):
-                t = raws.tile([P, PACK, LW], BF16, name="raw", align_bytes=64)
-                nc.sync.dma_start(out=t[:], in_=w1_view[g][:, :, j * LW : (j + 1) * LW])
-                w1_raw[g, j] = t
+            def load_w1(g, c):
+                t = raws.tile([P, PACK, CW], BF16, name="raw", align_bytes=64)
+                nc.sync.dma_start(out=t[:], in_=w1_view[g][:, :, c * CW : (c + 1) * CW])
+                w1_raw[g, c] = t
 
+            load_w2(0, 0, 1)
             h_sb = early.tile([P, 2, D], BF16)
             nc.sync.dma_start(out=h_sb[:], in_=h_attn.rearrange("b t d -> t b d"))
             wo_raw = {}
@@ -93,22 +93,39 @@ def tile_transformerblock_pa_kernel(
                 wo_raw[g, c] = t
 
             load_wo(0, 0)
-            load_w2(0, 0)
+            load_w2(1, 0, 1)
             load_wo(1, 0)
             load_wo(0, 1)
             load_wo(1, 1)
             x_sb = early.tile([P, 2, D], BF16)
             nc.sync.dma_start(out=x_sb[:], in_=x.rearrange("b t d -> t b d"))
-            load_w2(1, 0)
+
+            def spread(v):
+                t = early.tile([P, D], BF16, name="row%d" % len(rows))
+                nc.sync.dma_start(out=t[:], in_=v.partition_broadcast(P))
+                rows.append(t)
+
+            rows = []
+            spread(bo)
             load_w1(0, 0)
             load_w1(1, 0)
-            load_w2(0, 1)
-            load_w2(1, 1)
-            bias = const.tile([P, 2, F], BF16)
-            nc.sync.dma_start(out=bias[:, 0, :], in_=b1.partition_broadcast(P))
-            nc.sync.dma_start(out=bias[:, 1, :], in_=b2.partition_broadcast(P))
+            spread(ln2_g)
+            spread(ln2_b)
+            bo_sb, g2_sb, b2_sb = rows
+            load_w2(0, 1, 1)
+            load_w2(1, 1, 1)
             load_w1(0, 1)
             load_w1(1, 1)
+            load_w2(0, 2)
+            load_w2(1, 2)
+            bias = const.tile([P, 2, F], BF16)
+            for c in (2, 3):
+                load_w1(0, c)
+                load_w1(1, c)
+            for j in range(2):
+                cols = slice(j * (F // 2), (j + 1) * (F // 2))
+                nc.sync.dma_start(out=bias[:, 1, cols], in_=b2[cols].partition_broadcast(P))
+                nc.sync.dma_start(out=bias[:, 0, cols], in_=b1[cols].partition_broadcast(P))
 
             ident_b = const.tile([P, P], BF16)
             nc.vector.tensor_copy(out=ident_b[:], in_=ident[:])
@@ -147,33 +164,43 @@ def tile_transformerblock_pa_kernel(
             def do_widen(c, g, t):
                 if t == 0:
                     wide[c, g] = wides.tile([P, PACK, CW], BF16, name="wide", align_bytes=64)
-                cols = slice((c % 2) * CW, (c % 2 + 1) * CW)
                 nc.scalar.activation(
-                    out=wide[c, g][:, t, :], in_=w2_bytes[g, c // 2][:, t, cols].bitcast(FP8), func=ACT.Copy,
+                    out=wide[c, g][:, t, :], in_=w2_bytes[g, c][:, t, :].bitcast(FP8), func=ACT.Copy,
                     scale=scale_t[:, g, t : t + 1],
                 )
+
+            banks = []
+
+            def do_mm(n):
+                bank = ps_il.tile([P, 1024], BF16, name="bank")
+                base = n % 2 * 256
+                for k in range(2):
+                    nc.tensor.matmul(
+                        bank[:, k * 512 : (k + 1) * 512], lhsT=ident_b[:],
+                        rhs=w1_raw[1, n // 2][:, :, base + k * 128 : base + (k + 1) * 128].rearrange("p t w -> p w t"),
+                        start=True, stop=True,
+                    )
+                banks.append(bank)
 
             def do_il1(c, g, half):
                 if g == 0 and half == 0:
                     w_new(0, c)
-                base = (c % 2) * CW + half * 256
+                    while len(banks) < min(2 * c + 2, W1_PE):
+                        do_mm(len(banks))
+                base = half * 256
                 dst = pair[0, c][:, g, half * 1024 : (half + 1) * 1024]
-                src = w1_raw[g, c // 2][:, :, base : base + 256]
+                src = w1_raw[g, c][:, :, base : base + 256]
                 n = 2 * c + half
                 if g == 1 and n < W1_PE:
-                    bank = ps_il.tile([P, 1024], BF16, name="bank")
-                    for k in range(2):
-                        nc.tensor.matmul(
-                            bank[:, k * 512 : (k + 1) * 512], lhsT=ident_b[:],
-                            rhs=src[:, :, k * 128 : (k + 1) * 128].rearrange("p t w -> p w t"), start=True, stop=True,
-                        )
-                    nc.scalar.copy(out=dst, in_=bank[:])
+                    while len(banks) < min(n + 1, W1_PE):
+                        do_mm(len(banks))
+                    nc.scalar.copy(out=dst, in_=banks[n][:])
                 else:
                     interleave("V" if g == 1 and n >= W1_S else "S", dst, src)
 
-            def load_pair(c, load):
+            def load_pair(c, load, i):
                 for g in range(G):
-                    load(g, c // 2 + 2)
+                    load(g, i)
 
             def do_il2(c, g):
                 if g == 0:
@@ -194,8 +221,8 @@ def tile_transformerblock_pa_kernel(
                     for t in range(PACK):
                         s_steps.append((do_widen, c, g, t))
                     v_steps.append((len(s_steps), do_il2, c, g))
-                if c % 2 == 1 and c // 2 + 2 < F // LW:
-                    s_steps.append((load_pair, c, load_w2))
+                if c % 2 == 1 and c + 3 < NC_:
+                    s_steps.append((load_pair, c, load_w2, c + 3))
                 v_steps.append((len(s_steps), do_q, 1, c))
                 for g in range(G):
                     for half in range(2):
@@ -204,8 +231,8 @@ def tile_transformerblock_pa_kernel(
                 for half in range(2):
                     if 2 * c + half >= W1_S:
                         v_steps.append((len(s_steps), do_il1, c, 1, half))
-                if c % 2 == 1 and c // 2 + 2 < F // LW:
-                    s_steps.append((load_pair, c, load_w1))
+                if c + 4 < NC_:
+                    s_steps.append((load_pair, c, load_w1, c + 4))
                 v_steps.append((len(s_steps), do_q, 0, c))
 
             done = {"s": 0, "v": 0}
@@ -224,6 +251,8 @@ def tile_transformerblock_pa_kernel(
                         done["v"] += 1
                         advance_s(step[0] + ahead - done["s"])
                         step[1](*step[2:])
+
+            advance_s(N_0)
 
             hq = early.tile([P, G, TOK], U32, align_bytes=64)
             hs = early.tile([P, G, TOK], U8, align_bytes=64)
@@ -244,19 +273,6 @@ def tile_transformerblock_pa_kernel(
             for g in range(G):
                 quantize(hq[:, g, :], hs[:, g, :], hgs[g][:])
 
-            rows = []
-            for i in range(3):
-                bank = ps_il.tile([P, 1024], BF16, name="bank")
-                for k in range(2):
-                    nc.tensor.matmul(
-                        bank[:, k * 512 : (k + 1) * 512],
-                        lhsT=ident_b[:, 2 * i + k : 2 * i + k + 1].to_broadcast([P, P]), rhs=vec[:], start=True, stop=True,
-                    )
-                row = early.tile([P, D], BF16, name="row%d" % i)
-                nc.scalar.copy(out=row[:], in_=bank[:])
-                rows.append(row)
-            bo_sb, g2_sb, b2_sb = rows
-
             woq = early.tile([P, G, D], U32, align_bytes=64)
             wos = early.tile([P, G, D], U8, align_bytes=64)
             xb = early.tile([P, 2, D], F32)
@@ -273,6 +289,8 @@ def tile_transformerblock_pa_kernel(
                 nc.vector.tensor_tensor(out=xb[:, g, :], in0=x_sb[:, g, :], in1=bo_sb[:], op=ALU.add)
                 quantize(woq[:, g, :], wos[:, g, :], wo_il[g][:].rearrange("p g c -> p (g c)"))
 
+            do_mm(0)
+            do_mm(1)
             def sum_sq(src, m, nm, ss):
                 sq = early.tile([P, D], F32, name="sq")
                 nc.scalar.activation(
@@ -379,13 +397,13 @@ def tile_transformerblock_pa_kernel(
             nc.sync.dma_start(out=out_dram[w][m][:, c * CW : (c + 1) * CW], in_=ot[:])
 
         todo = [(do_out, w, c, m) for c in range(NC_) for w in (1, 0) for m in range(2)]
-        ready = []
+        made = []
         while todo:
             advance_v(1, AHEAD)
-            n = 0
             more = done["v"] < len(v_steps)
-            while todo and n < (2 if more else 4) and (todo[0][1], todo[0][2]) in ready:
-                todo[0][0](*todo[0][1:])
-                todo.pop(0)
-                n += 1
-            ready = list(q)
+            ready = [k for k in todo if (k[1], k[2]) in made]
+            n = len(ready) if not more else 2 if len(ready) > N_BACK else 1
+            for k in ready[:n]:
+                k[0](*k[1:])
+                todo.remove(k)
+            made = list(q)

@@ -15,27 +15,19 @@ ALU = mybir.AluOpType
 P = 128
 PACK = 4
 D = 1024
+G = D // (P * PACK)
 F = 4096
 TOK = 256
-G = 2
+M = TOK // P
 CW = 512
-NC_ = F // CW
-EARLY_C = 3
-LW = 1024
+CHUNKS = F // CW
 EPS = 1e-5
 
 FLOPS = 2 * TOK * D * (D + 2 * F)
 
-AHEAD = 12
-N_BACK = 4
-N_0 = 4
-N_A = 14
-N_B = 3
-V_A = 0
-V_B = 2
-V_C = 2
-W1_PE = 14
-W1_S = 15
+EARLY_CHUNKS = 3
+FAR = 4
+IDX_W1, IDX_W2 = 0, 1
 
 
 def tile_transformerblock_pa_kernel(
@@ -44,18 +36,19 @@ def tile_transformerblock_pa_kernel(
     nc = tc.nc
     with ExitStack() as ctx:
         const = ctx.enter_context(tc.tile_pool(name="const", bufs=1))
-        work = ctx.enter_context(tc.tile_pool(name="work", bufs=2))
-        raws = ctx.enter_context(tc.tile_pool(name="raws", bufs=8))
+        work = ctx.enter_context(tc.tile_pool(name="work", bufs=G))
+        raws = ctx.enter_context(tc.tile_pool(name="raws", bufs=FAR * G))
         byts = ctx.enter_context(tc.tile_pool(name="byts", bufs=6))
         wides = ctx.enter_context(tc.tile_pool(name="wides", bufs=4))
         ils = ctx.enter_context(tc.tile_pool(name="ils", bufs=2))
-        cods = ctx.enter_context(tc.tile_pool(name="cods", bufs=EARLY_C))
-        ps_mm = ctx.enter_context(tc.psum_pool(name="ps_mm", bufs=4))
+        codes_early = ctx.enter_context(tc.tile_pool(name="codes_early", bufs=EARLY_CHUNKS))
+        ps_mm = ctx.enter_context(tc.psum_pool(name="ps_mm", bufs=6))
         ps_tr = ctx.enter_context(tc.psum_pool(name="ps_tr", bufs=2))
-        ps_il = ctx.enter_context(tc.psum_pool(name="ps_il", bufs=2))
         ctx.enter_context(tc.manual_schedule())
 
         with tc.tile_pool(name="early", bufs=1) as early:
+            one = const.tile([P, 1], F32)
+            nc.vector.memset(one[:], 1.0)
             ident = const.tile([P, P], F32)
             make_identity(nc, ident[:])
             scale_t = const.tile([P, G, PACK], F32)
@@ -64,14 +57,17 @@ def tile_transformerblock_pa_kernel(
             nc.scalar.dma_start(out=fg_b[:], in_=fln_g.rearrange("(g p t) -> p g t", p=P, t=PACK))
             fb_b = const.tile([P, G, PACK], BF16)
             nc.scalar.dma_start(out=fb_b[:], in_=fln_b.rearrange("(g p t) -> p g t", p=P, t=PACK))
+            warm = const.tile([P, 1], F32)
+            nc.scalar.activation(out=warm[:], in_=one[:], func=ACT.Abs_reciprocal_sqrt)
 
             w1_view = W1.rearrange("(g p t) n -> g p t n", p=P, t=PACK)
             w2_view = W2_bytes.rearrange("(g p t) n -> g p t n", p=P, t=PACK)
             wo_view = Wo.rearrange("(g p t) n -> g p t n", p=P, t=PACK)
             w2_bytes = {}
             w1_raw = {}
+            wo_raw = {}
 
-            def load_w2(g, c, n=2):
+            def load_w2(g, c, n):
                 t = byts.tile([P, PACK, n * CW], U8, name="w2b", align_bytes=64)
                 nc.sync.dma_start(out=t[:], in_=w2_view[g][:, :, c * CW : (c + n) * CW])
                 for k in range(n):
@@ -82,53 +78,55 @@ def tile_transformerblock_pa_kernel(
                 nc.sync.dma_start(out=t[:], in_=w1_view[g][:, :, c * CW : (c + 1) * CW])
                 w1_raw[g, c] = t
 
-            load_w2(0, 0, 1)
-            h_sb = early.tile([P, 2, D], BF16)
-            nc.sync.dma_start(out=h_sb[:], in_=h_attn.rearrange("b t d -> t b d"))
-            wo_raw = {}
-
             def load_wo(g, c):
                 t = early.tile([P, PACK, CW], BF16, name="wo%d%d" % (g, c), align_bytes=64)
                 nc.sync.dma_start(out=t[:], in_=wo_view[g][:, :, c * CW : (c + 1) * CW])
                 wo_raw[g, c] = t
 
-            load_wo(0, 0)
-            load_w2(1, 0, 1)
-            load_wo(1, 0)
-            load_wo(0, 1)
-            load_wo(1, 1)
-            x_sb = early.tile([P, 2, D], BF16)
-            nc.sync.dma_start(out=x_sb[:], in_=x.rearrange("b t d -> t b d"))
-
-            def spread(v):
-                t = early.tile([P, D], BF16, name="row%d" % len(rows))
-                nc.sync.dma_start(out=t[:], in_=v.partition_broadcast(P))
-                rows.append(t)
-
-            rows = []
-            spread(bo)
-            load_w1(0, 0)
-            load_w1(1, 0)
-            spread(ln2_g)
-            spread(ln2_b)
-            bo_sb, g2_sb, b2_sb = rows
-            load_w2(0, 1, 1)
-            load_w2(1, 1, 1)
-            load_w1(0, 1)
-            load_w1(1, 1)
-            load_w2(0, 2)
-            load_w2(1, 2)
             bias = const.tile([P, 2, F], BF16)
-            for c in (2, 3):
-                load_w1(0, c)
-                load_w1(1, c)
-            for j in range(2):
-                cols = slice(j * (F // 2), (j + 1) * (F // 2))
-                nc.sync.dma_start(out=bias[:, 1, cols], in_=b2[cols].partition_broadcast(P))
-                nc.sync.dma_start(out=bias[:, 0, cols], in_=b1[cols].partition_broadcast(P))
+            h_sb = early.tile([P, M, D], BF16)
+            x_sb = early.tile([P, M, D], BF16)
+            bo_sb = early.tile([P, D], BF16)
+            g2_sb = early.tile([P, D], BF16)
+            b2_sb = early.tile([P, D], BF16)
 
-            ident_b = const.tile([P, P], BF16)
-            nc.vector.tensor_copy(out=ident_b[:], in_=ident[:])
+            def spread(tile, vec):
+                nc.sync.dma_start(out=tile[:], in_=vec.partition_broadcast(P))
+
+            def load_bias(w, j):
+                cols = slice(j * (F // 2), (j + 1) * (F // 2))
+                nc.sync.dma_start(out=bias[:, w, cols], in_=(b1, b2)[w][cols].partition_broadcast(P))
+
+            load_w2(0, 0, 1)
+            nc.sync.dma_start(out=h_sb[:, 1, :], in_=h_attn[1])
+            nc.sync.dma_start(out=h_sb[:, 0, :], in_=h_attn[0])
+            load_wo(0, 1)
+            load_wo(1, 0)
+            load_wo(0, 0)
+            load_wo(1, 1)
+            spread(bo_sb, bo)
+            load_w2(1, 0, 1)
+            load_w2(0, 1, 1)
+            nc.sync.dma_start(out=x_sb[:, 0, :], in_=x[0])
+            nc.sync.dma_start(out=x_sb[:, 1, :], in_=x[1])
+            load_w1(0, 0)
+            load_w2(1, 1, 1)
+            load_w1(1, 0)
+            spread(g2_sb, ln2_g)
+            load_w1(1, 1)
+            load_bias(IDX_W2, 0)
+            load_w1(0, 1)
+            load_w1(0, 2)
+            spread(b2_sb, ln2_b)
+            load_w2(0, 2, 2)
+            load_bias(IDX_W1, 0)
+            load_w2(1, 2, 2)
+            load_w1(1, 2)
+            load_bias(IDX_W2, 1)
+            load_w1(1, 3)
+            load_bias(IDX_W1, 1)
+            load_w1(0, 3)
+
             fg = const.tile([P, G, PACK], F32)
             nc.gpsimd.tensor_copy(out=fg[:], in_=fg_b[:])
             fb = const.tile([P, G, PACK], F32)
@@ -142,124 +140,132 @@ def tile_transformerblock_pa_kernel(
                 else:
                     nc.scalar.copy(out=o, in_=i)
 
-            def quantize(codes, scales, src):
-                nc.vector.quantize_mx(out=codes.bitcast(FP8X4), scales=scales, in_=src)
+            def quantize(code_out, scale_out, src):
+                nc.vector.quantize_mx(out=code_out.bitcast(FP8X4), scales=scale_out, in_=src)
 
-            def mx(acc, lc, ls, rc, rs, g):
-                nc.tensor.matmul_mx(
-                    out=acc, lhsT=lc.bitcast(FP8X4), lhsT_scale=ls, rhs=rc.bitcast(FP8X4), rhs_scale=rs,
-                    start=(g == 0), stop=(g == G - 1),
-                )
-
-            q = {}
-            s = {}
-            pair = {}
-            wide = {}
-            s_steps = []
-            v_steps = []
-
-            def w_new(w, c):
-                pair[w, c] = ils.tile([P, G, CW * PACK], BF16, name="il%d" % w, align_bytes=64)
-
-            def do_widen(c, g, t):
-                if t == 0:
-                    wide[c, g] = wides.tile([P, PACK, CW], BF16, name="wide", align_bytes=64)
-                nc.scalar.activation(
-                    out=wide[c, g][:, t, :], in_=w2_bytes[g, c][:, t, :].bitcast(FP8), func=ACT.Copy,
-                    scale=scale_t[:, g, t : t + 1],
-                )
-
-            banks = []
-
-            def do_mm(n):
-                bank = ps_il.tile([P, 1024], BF16, name="bank")
-                base = n % 2 * 256
-                for k in range(2):
-                    nc.tensor.matmul(
-                        bank[:, k * 512 : (k + 1) * 512], lhsT=ident_b[:],
-                        rhs=w1_raw[1, n // 2][:, :, base + k * 128 : base + (k + 1) * 128].rearrange("p t w -> p w t"),
-                        start=True, stop=True,
+            def product(acc, lhs_codes, lhs_scales, rhs_codes, rhs_scales, m, cols):
+                rows = slice(m * P, (m + 1) * P)
+                for g in range(G):
+                    nc.tensor.matmul_mx(
+                        out=acc[:],
+                        lhsT=lhs_codes[:, g, rows].bitcast(FP8X4),
+                        lhsT_scale=lhs_scales[:, g, rows],
+                        rhs=rhs_codes[:, g, cols].bitcast(FP8X4),
+                        rhs_scale=rhs_scales[:, g, cols],
+                        start=(g == 0),
+                        stop=(g == G - 1),
                     )
-                banks.append(bank)
 
-            def do_il1(c, g, half):
-                if g == 0 and half == 0:
-                    w_new(0, c)
-                    while len(banks) < min(2 * c + 2, W1_PE):
-                        do_mm(len(banks))
-                base = half * 256
-                dst = pair[0, c][:, g, half * 1024 : (half + 1) * 1024]
-                src = w1_raw[g, c][:, :, base : base + 256]
-                n = 2 * c + half
-                if g == 1 and n < W1_PE:
-                    while len(banks) < min(n + 1, W1_PE):
-                        do_mm(len(banks))
-                    nc.scalar.copy(out=dst, in_=banks[n][:])
-                else:
-                    interleave("V" if g == 1 and n >= W1_S else "S", dst, src)
-
-            def load_pair(c, load, i):
-                for g in range(G):
-                    load(g, i)
-
-            def do_il2(c, g):
-                if g == 0:
-                    w_new(1, c)
-                interleave("V", pair[1, c][:, g, :], wide[c, g][:])
-
-            def do_q(w, c):
-                pool = cods if c < EARLY_C else late
-                q[w, c] = pool.tile([P, G, CW], U32, name="q%d" % w, align_bytes=64)
-                s[w, c] = pool.tile([P, G, CW], U8, name="s%d" % w, align_bytes=64)
-                quantize(
-                    q[w, c][:].rearrange("p g c -> p (g c)"), s[w, c][:].rearrange("p g c -> p (g c)"),
-                    pair[w, c][:].rearrange("p g c -> p (g c)"),
-                )
-
-            for c in range(NC_):
-                for g in range(G):
-                    for t in range(PACK):
-                        s_steps.append((do_widen, c, g, t))
-                    v_steps.append((len(s_steps), do_il2, c, g))
-                if c % 2 == 1 and c + 3 < NC_:
-                    s_steps.append((load_pair, c, load_w2, c + 3))
-                v_steps.append((len(s_steps), do_q, 1, c))
-                for g in range(G):
-                    for half in range(2):
-                        if g == 0 or 2 * c + half < W1_S:
-                            s_steps.append((do_il1, c, g, half))
-                for half in range(2):
-                    if 2 * c + half >= W1_S:
-                        v_steps.append((len(s_steps), do_il1, c, 1, half))
-                if c + 4 < NC_:
-                    s_steps.append((load_pair, c, load_w1, c + 4))
-                v_steps.append((len(s_steps), do_q, 0, c))
-
+            codes = {}
+            scales = {}
+            made = set()
+            laid = {}
+            wide = {}
+            scalar_steps = []
+            vector_steps = []
             done = {"s": 0, "v": 0}
+            halves_left = [2 * G] * CHUNKS
 
             def advance_s(n):
                 for k in range(n):
-                    if done["s"] < len(s_steps):
-                        step = s_steps[done["s"]]
+                    if done["s"] < len(scalar_steps):
+                        step = scalar_steps[done["s"]]
                         done["s"] += 1
                         step[0](*step[1:])
 
-            def advance_v(n, ahead=0):
+            def advance_v(n):
                 for k in range(n):
-                    if done["v"] < len(v_steps):
-                        step = v_steps[done["v"]]
+                    if done["v"] < len(vector_steps):
+                        step = vector_steps[done["v"]]
                         done["v"] += 1
-                        advance_s(step[0] + ahead - done["s"])
+                        advance_s(step[0] - done["s"])
                         step[1](*step[2:])
 
-            advance_s(N_0)
+            def new_laid(w, c):
+                laid[w, c] = ils.tile([P, G, CW * PACK], BF16, name="il%d" % w, align_bytes=64)
+
+            def widen(c, g, t):
+                if t == 0:
+                    wide[c, g] = wides.tile([P, PACK, CW], BF16, name="wide", align_bytes=64)
+                nc.scalar.activation(
+                    out=wide[c, g][:, t, :],
+                    in_=w2_bytes[g, c][:, t, :].bitcast(FP8),
+                    func=ACT.Copy,
+                    scale=scale_t[:, g, t : t + 1],
+                )
+
+            def lay_w1(c, g, half, engine):
+                if halves_left[c] == 2 * G:
+                    new_laid(IDX_W1, c)
+                halves_left[c] -= 1
+                n = CW // 2
+                cols = slice(half * n, (half + 1) * n)
+                interleave(engine, laid[IDX_W1, c][:, g, half * n * PACK : (half + 1) * n * PACK], w1_raw[g, c][:, :, cols])
+
+            def lay_w2(c, g, engine):
+                if g == 0:
+                    new_laid(IDX_W2, c)
+                interleave(engine, laid[IDX_W2, c][:, g, :], wide[c, g][:])
+
+            def reload_w1(c):
+                while halves_left[c - FAR]:
+                    advance_v(1)
+                for g in range(G):
+                    load_w1(g, c)
+
+            def reload_w2(c):
+                for g in range(G):
+                    load_w2(g, c, 2)
+
+            def make_codes(w, c, passes):
+                if passes.start == 0:
+                    pool = codes_early if c < EARLY_CHUNKS else codes_late
+                    codes[w, c] = pool.tile([P, G, CW], U32, name="q%d" % w, align_bytes=64)
+                    scales[w, c] = pool.tile([P, G, CW], U8, name="s%d" % w, align_bytes=64)
+                quantize(
+                    codes[w, c][:, passes, :].rearrange("p g c -> p (g c)"),
+                    scales[w, c][:, passes, :].rearrange("p g c -> p (g c)"),
+                    laid[w, c][:, passes, :].rearrange("p g c -> p (g c)"),
+                )
+                if passes.stop == G:
+                    made.add((w, c))
+
+            def vector_lays_w1(c, g, half):
+                return g == 1 and c < (4, 7)[half]
+
+            both = slice(0, G)
+            pieces = [(g, half) for g in range(G) for half in range(2)]
+            for c in range(CHUNKS):
+                last = c == CHUNKS - 1
+                for g, half in pieces:
+                    if vector_lays_w1(c, g, half):
+                        vector_steps.append((len(scalar_steps), lay_w1, c, g, half, "V"))
+                for g in range(G):
+                    for t in range(PACK):
+                        scalar_steps.append((widen, c, g, t))
+                    if last and g == 0:
+                        scalar_steps.append((lay_w2, c, g, "S"))
+                    else:
+                        vector_steps.append((len(scalar_steps), lay_w2, c, g, "V"))
+                if c % 2 == 1 and c + 3 < CHUNKS:
+                    scalar_steps.append((reload_w2, c + 3))
+                vector_steps.append((len(scalar_steps), make_codes, IDX_W2, c, both))
+                for g, half in pieces:
+                    if not vector_lays_w1(c, g, half):
+                        scalar_steps.append((lay_w1, c, g, half, "S"))
+                    if last and (g, half) == (0, 1):
+                        vector_steps.append((len(scalar_steps), make_codes, IDX_W1, c, slice(0, 1)))
+                if c + FAR < CHUNKS:
+                    scalar_steps.append((reload_w1, c + FAR))
+                vector_steps.append((len(scalar_steps), make_codes, IDX_W1, c, slice(1, G) if last else both))
+
 
             hq = early.tile([P, G, TOK], U32, align_bytes=64)
             hs = early.tile([P, G, TOK], U8, align_bytes=64)
             hgs = []
             for g in range(G):
                 xt = ps_tr.tile([P, 2, TOK], F32, name="tr")
-                for m in range(2):
+                for m in range(M):
                     words = h_sb[:, m, :].bitcast(F32)
                     for u in range(2):
                         nc.tensor.transpose(
@@ -275,135 +281,160 @@ def tile_transformerblock_pa_kernel(
 
             woq = early.tile([P, G, D], U32, align_bytes=64)
             wos = early.tile([P, G, D], U8, align_bytes=64)
-            xb = early.tile([P, 2, D], F32)
-            wo_il = []
+            xb = early.tile([P, M, D], F32)
+            wo_laid = []
             for g in range(G):
-                pair_o = ils.tile([P, G, CW * PACK], BF16, name="il%d" % g, align_bytes=64)
-                wo_il.append(pair_o)
-            interleave("V", wo_il[0][:, 0, :], wo_raw[0, 0][:])
+                t = ils.tile([P, D // CW, CW * PACK], BF16, name="il%d" % g, align_bytes=64)
+                wo_laid.append(t)
+            interleave("V", wo_laid[0][:, 0, :], wo_raw[0, 0][:])
             advance_s(4)
-            interleave("V", wo_il[1][:, 0, :], wo_raw[1, 0][:])
-            interleave("V", wo_il[0][:, 1, :], wo_raw[0, 1][:])
-            interleave("S", wo_il[1][:, 1, :], wo_raw[1, 1][:])
+            interleave("V", wo_laid[1][:, 0, :], wo_raw[1, 0][:])
+            interleave("S", wo_laid[0][:, 1, :], wo_raw[0, 1][:])
+            interleave("S", wo_laid[1][:, 1, :], wo_raw[1, 1][:])
             for g in range(G):
-                nc.vector.tensor_tensor(out=xb[:, g, :], in0=x_sb[:, g, :], in1=bo_sb[:], op=ALU.add)
-                quantize(woq[:, g, :], wos[:, g, :], wo_il[g][:].rearrange("p g c -> p (g c)"))
+                quantize(woq[:, g, :], wos[:, g, :], wo_laid[g][:].rearrange("p c w -> p (c w)"))
+            advance_s(6)
+            for m in range(M):
+                nc.vector.tensor_tensor(out=xb[:, m, :], in0=x_sb[:, m, :], in1=bo_sb[:], op=ALU.add)
 
-            do_mm(0)
-            do_mm(1)
-            def sum_sq(src, m, nm, ss):
+            def sum_squares(src, m, neg_mean, total):
                 sq = early.tile([P, D], F32, name="sq")
                 nc.scalar.activation(
-                    out=sq[:], in_=src, func=ACT.Square, bias=nm[:, m : m + 1], accum_out=ss[:, m : m + 1]
+                    out=sq[:], in_=src, func=ACT.Square, bias=neg_mean[:, m : m + 1], accum_out=total[:, m : m + 1]
                 )
 
-            def rstd(ss, name):
-                ve = early.tile([P, 2], F32, name="ve" + name)
-                nc.vector.tensor_scalar(out=ve[:], in0=ss[:], scalar1=1.0 / D, scalar2=EPS, op0=ALU.mult, op1=ALU.add)
-                rs = early.tile([P, 2], F32, name="rs" + name)
-                nc.scalar.activation(out=rs[:], in_=ve[:], func=ACT.Abs_reciprocal_sqrt)
-                return rs
+            def inverse_deviation(total, name):
+                t = early.tile([P, M], F32, name=name)
+                nc.scalar.activation(out=t[:], in_=total[:], func=ACT.Abs_reciprocal_sqrt, scale=1.0 / D, bias=EPS)
+                return t
 
-            rr = []
-            sums = early.tile([P, 2, 2], F32)
-            nm1 = early.tile([P, 2], F32)
-            ss1 = early.tile([P, 2], F32)
-            for m in range(2):
-                y = xb[:, m, :]
+            sums = early.tile([P, 2, M], F32)
+            neg_mean1 = early.tile([P, M], F32)
+            squares1 = early.tile([P, M], F32)
+
+            def first_mean(m):
+                nc.vector.tensor_scalar(
+                    out=neg_mean1[:, m : m + 1],
+                    in0=sums[:, 0, m : m + 1],
+                    scalar1=sums[:, 1, m : m + 1],
+                    scalar2=-1.0 / D,
+                    op0=ALU.add,
+                    op1=ALU.mult,
+                )
+
+            for m in range(M):
                 for n in range(2):
-                    acc = ps_mm.tile([P, 512], F32, name="acc")
-                    cols = slice(n * 512, (n + 1) * 512)
-                    for g in range(G):
-                        mx(acc[:], hq[:, g, m * P : (m + 1) * P], hs[:, g, m * P : (m + 1) * P], woq[:, g, cols], wos[:, g, cols], g)
+                    acc = ps_mm.tile([P, CW], F32, name="acc")
+                    cols = slice(n * CW, (n + 1) * CW)
+                    product(acc, hq, hs, woq, wos, m, cols)
                     nc.vector.scalar_tensor_tensor(
-                        out=y[:, cols], in0=acc[:], scalar=1.0, in1=xb[:, m, cols], op0=ALU.mult, op1=ALU.add,
+                        out=xb[:, m, cols],
+                        in0=acc[:],
+                        scalar=1.0,
+                        in1=xb[:, m, cols],
+                        op0=ALU.mult,
+                        op1=ALU.add,
                         accum_out=sums[:, n, m : m + 1],
                     )
-            half = early.tile([P, 2], F32)
-            nc.vector.tensor_tensor(out=half[:], in0=sums[:, 0, :], in1=sums[:, 1, :], op=ALU.add)
-            nc.vector.tensor_scalar(out=nm1[:], in0=half[:], scalar1=-1.0 / D, scalar2=None, op0=ALU.mult)
-            advance_s(N_A)
-            for m in range(2):
-                sum_sq(xb[:, m, :], m, nm1, ss1)
-            for m in range(2):
-                y = xb[:, m, :]
-                t = early.tile([P, D], F32, name="t%d" % m)
+                    if (m, n) == (1, 0):
+                        first_mean(0)
+            advance_s(5)
+            rs = []
+            for m in range(M):
+                sum_squares(xb[:, m, :], m, neg_mean1, squares1)
+                r = early.tile([P, D], F32, name="r%d" % m)
                 nc.vector.scalar_tensor_tensor(
-                    out=t[:], in0=y, scalar=nm1[:, m : m + 1], in1=g2_sb[:], op0=ALU.add, op1=ALU.mult
+                    out=r[:], in0=xb[:, m, :], scalar=neg_mean1[:, m : m + 1], in1=g2_sb[:], op0=ALU.add, op1=ALU.mult
                 )
-                rr.append(t)
-            rs1 = rstd(ss1, "a")
-            sumr = early.tile([P, 2], F32)
-            nm2 = early.tile([P, 2], F32)
-            ss2 = early.tile([P, 2], F32)
-            advance_v(V_A)
-            for m in range(2):
-                r = rr[m][:]
+                rs.append(r)
+                if m == 0:
+                    first_mean(1)
+            inv1 = inverse_deviation(squares1, "inv1")
+            sum_r = early.tile([P, M], F32)
+            advance_v(2)
+            for m in range(M):
                 nc.vector.scalar_tensor_tensor(
-                    out=r, in0=r, scalar=rs1[:, m : m + 1], in1=b2_sb[:], op0=ALU.mult, op1=ALU.add,
-                    accum_out=sumr[:, m : m + 1],
+                    out=rs[m][:],
+                    in0=rs[m][:],
+                    scalar=inv1[:, m : m + 1],
+                    in1=b2_sb[:],
+                    op0=ALU.mult,
+                    op1=ALU.add,
+                    accum_out=sum_r[:, m : m + 1],
                 )
-                nc.sync.dma_start(out=out_0[m], in_=r)
-            nc.vector.tensor_scalar(out=nm2[:], in0=sumr[:], scalar1=-1.0 / D, scalar2=None, op0=ALU.mult)
-            advance_s(N_B)
-            for m in range(2):
-                sum_sq(rr[m][:], m, nm2, ss2)
-            advance_v(V_B)
-            rs2 = rstd(ss2, "b")
-            nb = early.tile([P, 2], F32)
-            nc.vector.tensor_tensor(out=nb[:], in0=nm2[:], in1=rs2[:], op=ALU.mult)
+                nc.sync.dma_start(out=out_0[m], in_=rs[m][:])
+
+            advance_s(11)
+            neg_mean2 = early.tile([P, M], F32)
+            squares2 = early.tile([P, M], F32)
+            nc.scalar.activation(out=neg_mean2[:], in_=sum_r[:], func=ACT.Copy, scale=-1.0 / D)
+            for m in range(M):
+                sum_squares(rs[m][:], m, neg_mean2, squares2)
+            advance_v(1)
+            inv2 = inverse_deviation(squares2, "inv2")
+            shift = early.tile([P, M], F32)
+            for m in range(M):
+                nc.scalar.activation(
+                    out=shift[:, m : m + 1], in_=neg_mean2[:, m : m + 1], func=ACT.Copy, scale=inv2[:, m : m + 1]
+                )
             zs = []
-            for m in range(2):
+            for m in range(M):
                 z = xb[:, m, :].rearrange("p (g t q) -> p g t q", g=G, t=PACK)
                 nc.scalar.activation(
-                    out=z, in_=rr[m][:].rearrange("p (g q t) -> p g t q", g=G, t=PACK), func=ACT.Identity,
-                    scale=rs2[:, m : m + 1], bias=nb[:, m : m + 1],
+                    out=z,
+                    in_=rs[m][:].rearrange("p (g q t) -> p g t q", g=G, t=PACK),
+                    func=ACT.Identity,
+                    scale=inv2[:, m : m + 1],
+                    bias=shift[:, m : m + 1],
                 )
                 zs.append(z)
-            advance_v(V_C)
+            advance_v(2)
 
             h2q = const.tile([P, G, TOK], U32, align_bytes=64)
             h2s = const.tile([P, G, TOK], U8, align_bytes=64)
-            his = []
+            h2_laid = []
             for g in range(G):
-                hT = work.tile([P, PACK, TOK], BF16, name="hT", align_bytes=64)
-                for tp in range(2):
+                h2 = work.tile([P, PACK, TOK], BF16, name="h2", align_bytes=64)
+                for tp in range(PACK // 2):
                     zt = ps_tr.tile([P, 2, TOK], F32, name="tr")
-                    for m in range(2):
+                    for m in range(M):
                         for u in range(2):
                             nc.tensor.transpose(zt[:, u, m * P : (m + 1) * P], zs[m][:, g, tp * 2 + u, :], ident[:])
                     for u in range(2):
                         t = tp * 2 + u
                         nc.scalar.activation(
-                            out=hT[:, t, :], in_=zt[:, u, :], func=ACT.Identity, scale=fg[:, g, t : t + 1], bias=fb[:, g, t : t + 1],
+                            out=h2[:, t, :],
+                            in_=zt[:, u, :],
+                            func=ACT.Identity,
+                            scale=fg[:, g, t : t + 1],
+                            bias=fb[:, g, t : t + 1],
                         )
                 advance_v(1)
-                hi = work.tile([P, TOK * PACK], BF16, name="hi", align_bytes=64)
-                interleave("V", hi[:], hT[:])
-                his.append(hi)
+                hl = work.tile([P, TOK * PACK], BF16, name="h2_laid", align_bytes=64)
+                interleave("V", hl[:], h2[:])
+                h2_laid.append(hl)
             for g in range(G):
-                quantize(h2q[:, g, :], h2s[:, g, :], his[g][:])
+                quantize(h2q[:, g, :], h2s[:, g, :], h2_laid[g][:])
 
         outs = ctx.enter_context(tc.tile_pool(name="outs", bufs=8))
-        late = ctx.enter_context(tc.tile_pool(name="late", bufs=4))
+        codes_late = ctx.enter_context(tc.tile_pool(name="late", bufs=4))
         out_dram = (out_1, out_2)
 
-        def do_out(w, c, m):
-            acc = ps_mm.tile([P, 512], F32, name="acc")
-            for g in range(G):
-                mx(acc[:], h2q[:, g, m * P : (m + 1) * P], h2s[:, g, m * P : (m + 1) * P], q[w, c][:, g, :], s[w, c][:, g, :], g)
+        def second_matmul(w, c, m):
+            acc = ps_mm.tile([P, CW], F32, name="acc")
+            product(acc, h2q, h2s, codes[w, c], scales[w, c], m, slice(0, CW))
             ot = outs.tile([P, CW], F32, name="ot")
-            nc.vector.tensor_tensor(out=ot[:], in0=acc[:], in1=bias[:, w, c * CW : (c + 1) * CW], op=ALU.add)
-            nc.sync.dma_start(out=out_dram[w][m][:, c * CW : (c + 1) * CW], in_=ot[:])
+            cols = slice(c * CW, (c + 1) * CW)
+            nc.vector.tensor_tensor(out=ot[:], in0=acc[:], in1=bias[:, w, cols], op=ALU.add)
+            nc.sync.dma_start(out=out_dram[w][m][:, cols], in_=ot[:])
 
-        todo = [(do_out, w, c, m) for c in range(NC_) for w in (1, 0) for m in range(2)]
-        made = []
+        todo = [(w, c, m) for c in range(CHUNKS) for w in (IDX_W2, IDX_W1) for m in range(M)]
+        complete = set()
         while todo:
-            advance_v(1, AHEAD)
-            more = done["v"] < len(v_steps)
-            ready = [k for k in todo if (k[1], k[2]) in made]
-            n = len(ready) if not more else 2 if len(ready) > N_BACK else 1
+            advance_v(1)
+            ready = [k for k in todo if k[:2] in complete]
+            n = len(ready) if done["v"] == len(vector_steps) else 2 if len(ready) > 10 else 1
             for k in ready[:n]:
-                k[0](*k[1:])
+                second_matmul(*k)
                 todo.remove(k)
-            made = list(q)
+            complete = set(made)

from contextlib import ExitStack

import concourse.mybir as mybir
from concourse.masks import make_identity

F32 = mybir.dt.float32
BF16 = mybir.dt.bfloat16
U32 = mybir.dt.uint32
U8 = mybir.dt.uint8
FP8 = mybir.dt.float8_e4m3fn
FP8X4 = mybir.dt.float8_e4m3fn_x4
ACT = mybir.ActivationFunctionType
ALU = mybir.AluOpType

P = 128
PACK = 4
D = 1024
G = D // (P * PACK)
F = 4096
TOK = 256
M = TOK // P
CW = 512
CHUNKS = F // CW
EPS = 1e-5

FLOPS = 2 * TOK * D * (D + 2 * F)

EARLY_CHUNKS = 3
FAR = 4
IDX_W1, IDX_W2 = 0, 1


def tile_transformerblock_pa_kernel(
    tc, h_attn, x, Wo, bo, ln2_g, ln2_b, fln_g, fln_b, W1, b1, W2_bytes, W2_scale, b2, out_0, out_1, out_2
):
    nc = tc.nc
    with ExitStack() as ctx:
        const = ctx.enter_context(tc.tile_pool(name="const", bufs=1))
        work = ctx.enter_context(tc.tile_pool(name="work", bufs=G))
        raws = ctx.enter_context(tc.tile_pool(name="raws", bufs=FAR * G))
        byts = ctx.enter_context(tc.tile_pool(name="byts", bufs=6))
        wides = ctx.enter_context(tc.tile_pool(name="wides", bufs=4))
        ils = ctx.enter_context(tc.tile_pool(name="ils", bufs=2))
        codes_early = ctx.enter_context(tc.tile_pool(name="codes_early", bufs=EARLY_CHUNKS))
        ps_mm = ctx.enter_context(tc.psum_pool(name="ps_mm", bufs=6))
        ps_tr = ctx.enter_context(tc.psum_pool(name="ps_tr", bufs=2))
        ctx.enter_context(tc.manual_schedule())

        with tc.tile_pool(name="early", bufs=1) as early:
            one = const.tile([P, 1], F32)
            nc.vector.memset(one[:], 1.0)
            ident = const.tile([P, P], F32)
            make_identity(nc, ident[:])
            scale_t = const.tile([P, G, PACK], F32)
            nc.scalar.dma_start(out=scale_t[:], in_=W2_scale.rearrange("(g p t) o -> p g (t o)", p=P, t=PACK))
            fg_b = const.tile([P, G, PACK], BF16)
            nc.scalar.dma_start(out=fg_b[:], in_=fln_g.rearrange("(g p t) -> p g t", p=P, t=PACK))
            fb_b = const.tile([P, G, PACK], BF16)
            nc.scalar.dma_start(out=fb_b[:], in_=fln_b.rearrange("(g p t) -> p g t", p=P, t=PACK))
            warm = const.tile([P, 1], F32)
            nc.scalar.activation(out=warm[:], in_=one[:], func=ACT.Abs_reciprocal_sqrt)

            w1_view = W1.rearrange("(g p t) n -> g p t n", p=P, t=PACK)
            w2_view = W2_bytes.rearrange("(g p t) n -> g p t n", p=P, t=PACK)
            wo_view = Wo.rearrange("(g p t) n -> g p t n", p=P, t=PACK)
            w2_bytes = {}
            w1_raw = {}
            wo_raw = {}

            def load_w2(g, c, n):
                t = byts.tile([P, PACK, n * CW], U8, name="w2b", align_bytes=64)
                nc.sync.dma_start(out=t[:], in_=w2_view[g][:, :, c * CW : (c + n) * CW])
                for k in range(n):
                    w2_bytes[g, c + k] = t[:, :, k * CW : (k + 1) * CW]

            def load_w1(g, c):
                t = raws.tile([P, PACK, CW], BF16, name="raw", align_bytes=64)
                nc.sync.dma_start(out=t[:], in_=w1_view[g][:, :, c * CW : (c + 1) * CW])
                w1_raw[g, c] = t

            def load_wo(g, c):
                t = early.tile([P, PACK, CW], BF16, name="wo%d%d" % (g, c), align_bytes=64)
                nc.sync.dma_start(out=t[:], in_=wo_view[g][:, :, c * CW : (c + 1) * CW])
                wo_raw[g, c] = t

            bias = const.tile([P, 2, F], BF16)
            h_sb = early.tile([P, M, D], BF16)
            x_sb = early.tile([P, M, D], BF16)
            bo_sb = early.tile([P, D], BF16)
            g2_sb = early.tile([P, D], BF16)
            b2_sb = early.tile([P, D], BF16)

            def spread(tile, vec):
                nc.sync.dma_start(out=tile[:], in_=vec.partition_broadcast(P))

            def load_bias(w, j):
                cols = slice(j * (F // 2), (j + 1) * (F // 2))
                nc.sync.dma_start(out=bias[:, w, cols], in_=(b1, b2)[w][cols].partition_broadcast(P))

            load_w2(0, 0, 1)
            nc.sync.dma_start(out=h_sb[:, 1, :], in_=h_attn[1])
            nc.sync.dma_start(out=h_sb[:, 0, :], in_=h_attn[0])
            load_wo(0, 1)
            load_wo(1, 0)
            load_wo(0, 0)
            load_wo(1, 1)
            spread(bo_sb, bo)
            load_w2(1, 0, 1)
            load_w2(0, 1, 1)
            nc.sync.dma_start(out=x_sb[:, 0, :], in_=x[0])
            nc.sync.dma_start(out=x_sb[:, 1, :], in_=x[1])
            load_w1(0, 0)
            load_w2(1, 1, 1)
            load_w1(1, 0)
            spread(g2_sb, ln2_g)
            load_w1(1, 1)
            load_bias(IDX_W2, 0)
            load_w1(0, 1)
            load_w1(0, 2)
            spread(b2_sb, ln2_b)
            load_w2(0, 2, 2)
            load_bias(IDX_W1, 0)
            load_w2(1, 2, 2)
            load_w1(1, 2)
            load_bias(IDX_W2, 1)
            load_w1(1, 3)
            load_bias(IDX_W1, 1)
            load_w1(0, 3)

            fg = const.tile([P, G, PACK], F32)
            nc.gpsimd.tensor_copy(out=fg[:], in_=fg_b[:])
            fb = const.tile([P, G, PACK], F32)
            nc.gpsimd.tensor_copy(out=fb[:], in_=fb_b[:])

            def interleave(engine, dst, src):
                o = dst.rearrange("p (c i t) -> p c t i", i=4, t=PACK)
                i = src.rearrange("p t (c i) -> p c t i", i=4)
                if engine == "V":
                    nc.vector.tensor_copy(out=o, in_=i)
                else:
                    nc.scalar.copy(out=o, in_=i)

            def quantize(code_out, scale_out, src):
                nc.vector.quantize_mx(out=code_out.bitcast(FP8X4), scales=scale_out, in_=src)

            def product(acc, lhs_codes, lhs_scales, rhs_codes, rhs_scales, m, cols):
                rows = slice(m * P, (m + 1) * P)
                for g in range(G):
                    nc.tensor.matmul_mx(
                        out=acc[:],
                        lhsT=lhs_codes[:, g, rows].bitcast(FP8X4),
                        lhsT_scale=lhs_scales[:, g, rows],
                        rhs=rhs_codes[:, g, cols].bitcast(FP8X4),
                        rhs_scale=rhs_scales[:, g, cols],
                        start=(g == 0),
                        stop=(g == G - 1),
                    )

            codes = {}
            scales = {}
            made = set()
            laid = {}
            wide = {}
            scalar_steps = []
            vector_steps = []
            done = {"s": 0, "v": 0}
            halves_left = [2 * G] * CHUNKS

            def advance_s(n):
                for k in range(n):
                    if done["s"] < len(scalar_steps):
                        step = scalar_steps[done["s"]]
                        done["s"] += 1
                        step[0](*step[1:])

            def advance_v(n):
                for k in range(n):
                    if done["v"] < len(vector_steps):
                        step = vector_steps[done["v"]]
                        done["v"] += 1
                        advance_s(step[0] - done["s"])
                        step[1](*step[2:])

            def new_laid(w, c):
                laid[w, c] = ils.tile([P, G, CW * PACK], BF16, name="il%d" % w, align_bytes=64)

            def widen(c, g, t):
                if t == 0:
                    wide[c, g] = wides.tile([P, PACK, CW], BF16, name="wide", align_bytes=64)
                nc.scalar.activation(
                    out=wide[c, g][:, t, :],
                    in_=w2_bytes[g, c][:, t, :].bitcast(FP8),
                    func=ACT.Copy,
                    scale=scale_t[:, g, t : t + 1],
                )

            def lay_w1(c, g, half, engine):
                if halves_left[c] == 2 * G:
                    new_laid(IDX_W1, c)
                halves_left[c] -= 1
                n = CW // 2
                cols = slice(half * n, (half + 1) * n)
                interleave(engine, laid[IDX_W1, c][:, g, half * n * PACK : (half + 1) * n * PACK], w1_raw[g, c][:, :, cols])

            def lay_w2(c, g, engine):
                if g == 0:
                    new_laid(IDX_W2, c)
                interleave(engine, laid[IDX_W2, c][:, g, :], wide[c, g][:])

            def reload_w1(c):
                while halves_left[c - FAR]:
                    advance_v(1)
                for g in range(G):
                    load_w1(g, c)

            def reload_w2(c):
                for g in range(G):
                    load_w2(g, c, 2)

            def make_codes(w, c, passes):
                if passes.start == 0:
                    pool = codes_early if c < EARLY_CHUNKS else codes_late
                    codes[w, c] = pool.tile([P, G, CW], U32, name="q%d" % w, align_bytes=64)
                    scales[w, c] = pool.tile([P, G, CW], U8, name="s%d" % w, align_bytes=64)
                quantize(
                    codes[w, c][:, passes, :].rearrange("p g c -> p (g c)"),
                    scales[w, c][:, passes, :].rearrange("p g c -> p (g c)"),
                    laid[w, c][:, passes, :].rearrange("p g c -> p (g c)"),
                )
                if passes.stop == G:
                    made.add((w, c))

            def vector_lays_w1(c, g, half):
                return g == 1 and c < (4, 7)[half]

            both = slice(0, G)
            pieces = [(g, half) for g in range(G) for half in range(2)]
            for c in range(CHUNKS):
                last = c == CHUNKS - 1
                for g, half in pieces:
                    if vector_lays_w1(c, g, half):
                        vector_steps.append((len(scalar_steps), lay_w1, c, g, half, "V"))
                for g in range(G):
                    for t in range(PACK):
                        scalar_steps.append((widen, c, g, t))
                    if last and g == 0:
                        scalar_steps.append((lay_w2, c, g, "S"))
                    else:
                        vector_steps.append((len(scalar_steps), lay_w2, c, g, "V"))
                if c % 2 == 1 and c + 3 < CHUNKS:
                    scalar_steps.append((reload_w2, c + 3))
                vector_steps.append((len(scalar_steps), make_codes, IDX_W2, c, both))
                for g, half in pieces:
                    if not vector_lays_w1(c, g, half):
                        scalar_steps.append((lay_w1, c, g, half, "S"))
                    if last and (g, half) == (0, 1):
                        vector_steps.append((len(scalar_steps), make_codes, IDX_W1, c, slice(0, 1)))
                if c + FAR < CHUNKS:
                    scalar_steps.append((reload_w1, c + FAR))
                vector_steps.append((len(scalar_steps), make_codes, IDX_W1, c, slice(1, G) if last else both))


            hq = early.tile([P, G, TOK], U32, align_bytes=64)
            hs = early.tile([P, G, TOK], U8, align_bytes=64)
            hgs = []
            for g in range(G):
                xt = ps_tr.tile([P, 2, TOK], F32, name="tr")
                for m in range(M):
                    words = h_sb[:, m, :].bitcast(F32)
                    for u in range(2):
                        nc.tensor.transpose(
                            xt[:, u, m * P : (m + 1) * P], words[:, 256 * g + u : 256 * (g + 1) : 2], ident[:]
                        )
                hg = early.tile([P, TOK * PACK], BF16, name="hg%d" % g, align_bytes=64)
                nc.vector.tensor_copy(
                    out=hg[:].bitcast(F32).rearrange("p (r u) -> p r u", u=2), in_=xt[:].rearrange("p u r -> p r u")
                )
                hgs.append(hg)
            for g in range(G):
                quantize(hq[:, g, :], hs[:, g, :], hgs[g][:])

            woq = early.tile([P, G, D], U32, align_bytes=64)
            wos = early.tile([P, G, D], U8, align_bytes=64)
            xb = early.tile([P, M, D], F32)
            wo_laid = []
            for g in range(G):
                t = ils.tile([P, D // CW, CW * PACK], BF16, name="il%d" % g, align_bytes=64)
                wo_laid.append(t)
            interleave("V", wo_laid[0][:, 0, :], wo_raw[0, 0][:])
            advance_s(4)
            interleave("V", wo_laid[1][:, 0, :], wo_raw[1, 0][:])
            interleave("S", wo_laid[0][:, 1, :], wo_raw[0, 1][:])
            interleave("S", wo_laid[1][:, 1, :], wo_raw[1, 1][:])
            for g in range(G):
                quantize(woq[:, g, :], wos[:, g, :], wo_laid[g][:].rearrange("p c w -> p (c w)"))
            advance_s(6)
            for m in range(M):
                nc.vector.tensor_tensor(out=xb[:, m, :], in0=x_sb[:, m, :], in1=bo_sb[:], op=ALU.add)

            def sum_squares(src, m, neg_mean, total):
                sq = early.tile([P, D], F32, name="sq")
                nc.scalar.activation(
                    out=sq[:], in_=src, func=ACT.Square, bias=neg_mean[:, m : m + 1], accum_out=total[:, m : m + 1]
                )

            def inverse_deviation(total, name):
                t = early.tile([P, M], F32, name=name)
                nc.scalar.activation(out=t[:], in_=total[:], func=ACT.Abs_reciprocal_sqrt, scale=1.0 / D, bias=EPS)
                return t

            sums = early.tile([P, 2, M], F32)
            neg_mean1 = early.tile([P, M], F32)
            squares1 = early.tile([P, M], F32)

            def first_mean(m):
                nc.vector.tensor_scalar(
                    out=neg_mean1[:, m : m + 1],
                    in0=sums[:, 0, m : m + 1],
                    scalar1=sums[:, 1, m : m + 1],
                    scalar2=-1.0 / D,
                    op0=ALU.add,
                    op1=ALU.mult,
                )

            for m in range(M):
                for n in range(2):
                    acc = ps_mm.tile([P, CW], F32, name="acc")
                    cols = slice(n * CW, (n + 1) * CW)
                    product(acc, hq, hs, woq, wos, m, cols)
                    nc.vector.scalar_tensor_tensor(
                        out=xb[:, m, cols],
                        in0=acc[:],
                        scalar=1.0,
                        in1=xb[:, m, cols],
                        op0=ALU.mult,
                        op1=ALU.add,
                        accum_out=sums[:, n, m : m + 1],
                    )
                    if (m, n) == (1, 0):
                        first_mean(0)
            advance_s(5)
            rs = []
            for m in range(M):
                sum_squares(xb[:, m, :], m, neg_mean1, squares1)
                r = early.tile([P, D], F32, name="r%d" % m)
                nc.vector.scalar_tensor_tensor(
                    out=r[:], in0=xb[:, m, :], scalar=neg_mean1[:, m : m + 1], in1=g2_sb[:], op0=ALU.add, op1=ALU.mult
                )
                rs.append(r)
                if m == 0:
                    first_mean(1)
            inv1 = inverse_deviation(squares1, "inv1")
            sum_r = early.tile([P, M], F32)
            advance_v(2)
            for m in range(M):
                nc.vector.scalar_tensor_tensor(
                    out=rs[m][:],
                    in0=rs[m][:],
                    scalar=inv1[:, m : m + 1],
                    in1=b2_sb[:],
                    op0=ALU.mult,
                    op1=ALU.add,
                    accum_out=sum_r[:, m : m + 1],
                )
                nc.sync.dma_start(out=out_0[m], in_=rs[m][:])

            advance_s(11)
            neg_mean2 = early.tile([P, M], F32)
            squares2 = early.tile([P, M], F32)
            nc.scalar.activation(out=neg_mean2[:], in_=sum_r[:], func=ACT.Copy, scale=-1.0 / D)
            for m in range(M):
                sum_squares(rs[m][:], m, neg_mean2, squares2)
            advance_v(1)
            inv2 = inverse_deviation(squares2, "inv2")
            shift = early.tile([P, M], F32)
            for m in range(M):
                nc.scalar.activation(
                    out=shift[:, m : m + 1], in_=neg_mean2[:, m : m + 1], func=ACT.Copy, scale=inv2[:, m : m + 1]
                )
            zs = []
            for m in range(M):
                z = xb[:, m, :].rearrange("p (g t q) -> p g t q", g=G, t=PACK)
                nc.scalar.activation(
                    out=z,
                    in_=rs[m][:].rearrange("p (g q t) -> p g t q", g=G, t=PACK),
                    func=ACT.Identity,
                    scale=inv2[:, m : m + 1],
                    bias=shift[:, m : m + 1],
                )
                zs.append(z)
            advance_v(2)

            h2q = const.tile([P, G, TOK], U32, align_bytes=64)
            h2s = const.tile([P, G, TOK], U8, align_bytes=64)
            h2_laid = []
            for g in range(G):
                h2 = work.tile([P, PACK, TOK], BF16, name="h2", align_bytes=64)
                for tp in range(PACK // 2):
                    zt = ps_tr.tile([P, 2, TOK], F32, name="tr")
                    for m in range(M):
                        for u in range(2):
                            nc.tensor.transpose(zt[:, u, m * P : (m + 1) * P], zs[m][:, g, tp * 2 + u, :], ident[:])
                    for u in range(2):
                        t = tp * 2 + u
                        nc.scalar.activation(
                            out=h2[:, t, :],
                            in_=zt[:, u, :],
                            func=ACT.Identity,
                            scale=fg[:, g, t : t + 1],
                            bias=fb[:, g, t : t + 1],
                        )
                advance_v(1)
                hl = work.tile([P, TOK * PACK], BF16, name="h2_laid", align_bytes=64)
                interleave("V", hl[:], h2[:])
                h2_laid.append(hl)
            for g in range(G):
                quantize(h2q[:, g, :], h2s[:, g, :], h2_laid[g][:])

        outs = ctx.enter_context(tc.tile_pool(name="outs", bufs=8))
        codes_late = ctx.enter_context(tc.tile_pool(name="late", bufs=4))
        out_dram = (out_1, out_2)

        def second_matmul(w, c, m):
            acc = ps_mm.tile([P, CW], F32, name="acc")
            product(acc, h2q, h2s, codes[w, c], scales[w, c], m, slice(0, CW))
            ot = outs.tile([P, CW], F32, name="ot")
            cols = slice(c * CW, (c + 1) * CW)
            nc.vector.tensor_tensor(out=ot[:], in0=acc[:], in1=bias[:, w, cols], op=ALU.add)
            nc.sync.dma_start(out=out_dram[w][m][:, cols], in_=ot[:])

        todo = [(w, c, m) for c in range(CHUNKS) for w in (IDX_W2, IDX_W1) for m in range(M)]
        complete = set()
        while todo:
            advance_v(1)
            ready = [k for k in todo if k[:2] in complete]
            n = len(ready) if done["v"] == len(vector_steps) else 2 if len(ready) > 10 else 1
            for k in ready[:n]:
                second_matmul(*k)
                todo.remove(k)
            complete = set(made)
